import numpy as np
import ml_dtypes


def mxq(x, axis, fmt="e4m3"):
    dtype, down = {"e4m3": (ml_dtypes.float8_e4m3fn, 7), "e5m2": (ml_dtypes.float8_e5m2, 14)}[fmt]
    v = np.moveaxis(np.asarray(x, np.float32).astype(ml_dtypes.bfloat16).astype(np.float64), axis, -1)
    blocks = v.reshape(v.shape[:-1] + (-1, 32))
    amax = np.abs(blocks).max(-1, keepdims=True)
    byte = np.maximum(np.where(amax > 0, np.frexp(amax)[1] - 1 + 127, 0) - down, 1)
    scale = np.exp2(byte - 127.0)
    codes = (blocks / scale).astype(np.float32).astype(dtype).astype(np.float64)
    return np.moveaxis((codes * scale).reshape(v.shape), -1, axis)


WIDE = False


def mx_kscale(k):
    if not WIDE:
        return np.ones(k)
    levels = np.array([10, -10, 5, -5, 0])
    a = np.random.permutation(np.resize(levels, k // 512 * 4)).reshape(k // 512, 4)
    idx = np.arange(k)
    return np.exp2(a[idx // 512, idx % 128 // 32])


BF16 = ml_dtypes.bfloat16


def bf(x):
    return np.asarray(x, np.float32).astype(BF16)


def f64(x):
    return np.asarray(x).astype(np.float64)


B, IN, HID = 4096, 512, 512


def sigmoid(v):
    return 1.0 / (1.0 + np.exp(-v))


def lin(xq, w):
    return xq @ mxq(f64(w), 1, "e4m3").T


def setup_inputs():
    s, p = mx_kscale(IN), mx_kscale(HID)
    return {"inputs": bf(np.random.standard_normal((B, IN)) * s),
            "state": bf(np.random.standard_normal((B, HID))),
            "parent_state": bf(np.random.standard_normal((B, HID)) * p),
            "c": bf(np.tanh(np.random.standard_normal((B, HID)))),
            "w_a_w": bf(np.random.standard_normal((HID, IN)) * 0.6 / np.sqrt(IN) / s),
            "w_a_b": bf(np.random.standard_normal(HID) * 0.5),
            "u_a_w": bf(np.random.standard_normal((HID, HID)) * 0.6 / np.sqrt(HID)),
            "p_a_w": bf(np.random.standard_normal((HID, HID)) * 0.6 / np.sqrt(HID) / p)}


def reference(inputs, state, parent_state, c, w_a_w, w_a_b, u_a_w, p_a_w):
    st = f64(state)
    att = sigmoid(lin(mxq(f64(inputs), 1, "e4m3"), w_a_w) + f64(w_a_b) + lin(mxq(st, 1, "e4m3"), u_a_w) + lin(mxq(f64(parent_state), 1, "e4m3"), p_a_w))
    return att * f64(c) + (1.0 - att) * st

@@ -1,0 +1,233 @@
+from contextlib import ExitStack
+
+import concourse.mybir as mybir
+from concourse.masks import make_identity
+
+F32 = mybir.dt.float32
+BF16 = mybir.dt.bfloat16
+U32 = mybir.dt.uint32
+U8 = mybir.dt.uint8
+FP8X4 = mybir.dt.float8_e4m3fn_x4
+ACT = mybir.ActivationFunctionType
+ALU = mybir.AluOpType
+
+P = 128
+B, K, H = 4096, 512, 512
+R = 4
+CH = P * R
+NCH = B // CH
+FLOPS = 2 * B * 3 * K * H
+
+PIN = False
+G_ROWTILES = 0
+PRELOAD = 4
+D_AHEAD = 2
+TXPLAN = {0: (1,), 1: (2, 3), 2: (4,), 3: (5,), 4: (6,), 5: (7,)}
+
+
+def tile_parentgru_pb_t_kernel(tc, inputs, state, parent_state, c, w_a_w, w_a_b, u_a_w, p_a_w, out):
+    nc = tc.nc
+    acts = (inputs, state, parent_state)
+    weights = (w_a_w, u_a_w, p_a_w)
+    with ExitStack() as ctx:
+        if PIN:
+            ctx.enter_context(tc.manual_schedule())
+        const = ctx.enter_context(tc.tile_pool(name="const", bufs=1))
+        xpool = ctx.enter_context(tc.tile_pool(name="xpool", bufs=3))
+        spool = ctx.enter_context(tc.tile_pool(name="spool", bufs=6))
+        cpool = ctx.enter_context(tc.tile_pool(name="cpool", bufs=4))
+        bpool = ctx.enter_context(tc.tile_pool(name="bpool", bufs=5))
+        gpool = ctx.enter_context(tc.tile_pool(name="gpool", bufs=4))
+        qpool = ctx.enter_context(tc.tile_pool(name="qpool", bufs=3))
+        apool = ctx.enter_context(tc.tile_pool(name="apool", bufs=2))
+        psx = ctx.enter_context(tc.psum_pool(name="psx", bufs=2))
+        psz = ctx.enter_context(tc.psum_pool(name="psz", bufs=4))
+        psa = ctx.enter_context(tc.psum_pool(name="psa", bufs=2))
+
+        ident = const.tile([P, P], F32, name="ident")
+        make_identity(nc, ident[:])
+        warm = const.tile([P, 1], F32, name="warm")
+        warmed = const.tile([P, 1], F32, name="warmed")
+        nc.vector.memset(warm[:], 0.0)
+        nc.scalar.activation(out=warmed[:], in_=warm[:], func=ACT.Sigmoid)
+        braw = const.tile([P, P], BF16, name="braw")
+        nc.vector.memset(braw[:], 0.0)
+        nc.scalar.dma_start(out=braw[0:4, :], in_=w_a_b.rearrange("(m p) -> m p", p=P))
+
+        xt_sb = {}
+        c_sb = {}
+        blend = {}
+        codes = {}
+        planes = {}
+        att_t = {}
+        w_sb = []
+        w_codes = []
+        w_planes = []
+
+        def rows(ap, j):
+            return ap[j * CH : (j + 1) * CH, :].rearrange("(p r) k -> p (r k)", r=R)
+
+        def load_w(i):
+            t = const.tile([P, R, K], BF16, name="w%d" % i)
+            nc.sync.dma_start(out=t[:], in_=weights[i].rearrange("(m p) k -> p m k", p=P))
+            w_sb.append(t)
+
+        def load_x(j, i):
+            pool = spool if i == 1 else xpool
+            t = pool.tile([P, R * K], BF16, name="x%d_%d" % (i, j), tag="x%d" % i)
+            nc.sync.dma_start(out=t[:], in_=rows(acts[i], j))
+            xt_sb[(j, i)] = t
+
+        def load_c(j):
+            t = cpool.tile([P, R * K], BF16, name="c_%d" % j, tag="c")
+            nc.sync.dma_start(out=t[:], in_=rows(c, j))
+            c_sb[j] = t
+
+        def load_chunk(j):
+            for i in range(3):
+                load_x(j, i)
+            load_c(j)
+
+        def flip_pair(words, half, g32, on_vector):
+            bank = psx.tile([P, 2, 2 * P], F32, name="bank", tag="xt")
+            for rr in range(2):
+                for u in range(2):
+                    col = (2 * half + rr) * (K // 2) + u * P
+                    nc.tensor.transpose(bank[:, u, rr * P : (rr + 1) * P], words[:, col : col + P], ident[:])
+            dst = g32[:, half * 2 * P : (half + 1) * 2 * P, :]
+            src = bank[:].rearrange("q u n -> q n u")
+            if on_vector:
+                nc.vector.tensor_copy(out=dst, in_=src)
+            else:
+                nc.scalar.copy(out=dst, in_=src)
+
+        def new_grouped(label):
+            g = gpool.tile([P, 4 * CH], BF16, name="g" + label, tag="g", align_bytes=64)
+            return g, g[:].bitcast(F32).rearrange("q (n u) -> q n u", u=2)
+
+        def quantise(g, cd, pl):
+            nc.vector.quantize_mx(out=cd[:].bitcast(FP8X4), scales=pl[:], in_=g[:])
+
+        def prep_w(i):
+            g, g32 = new_grouped("w%d" % i)
+            words = w_sb[i][:].rearrange("p m k -> p (m k)").bitcast(F32)
+            for half in range(2):
+                flip_pair(words, half, g32, True)
+            cd = const.tile([P, H], U32, name="wc%d" % i, align_bytes=64)
+            pl = const.tile([P, H], U8, name="wp%d" % i, align_bytes=64)
+            quantise(g, cd, pl)
+            w_codes.append(cd)
+            w_planes.append(pl)
+
+        def flip_jobs(j):
+            jobs = []
+            for i in range(3):
+                box = {}
+
+                def first(i=i, box=box):
+                    box["g"] = new_grouped("x%d_%d" % (i, j))
+                    flip_pair(xt_sb[(j, i)][:].bitcast(F32), 0, box["g"][1], False)
+
+                def second(i=i, box=box):
+                    flip_pair(xt_sb[(j, i)][:].bitcast(F32), 1, box["g"][1], False)
+                    cd = qpool.tile([P, CH], U32, name="xc%d_%d" % (i, j), tag="xc%d" % i, align_bytes=64)
+                    pl = qpool.tile([P, CH], U8, name="xp%d_%d" % (i, j), tag="xp%d" % i, align_bytes=64)
+                    quantise(box["g"][0], cd, pl)
+                    codes[(j, i)] = cd
+                    planes[(j, i)] = pl
+
+                jobs.append(first)
+                jobs.append(second)
+            return jobs
+
+        def dsub(j):
+            t = bpool.tile([P, R * H], F32, name="bl_%d" % j, tag="bl")
+            cut = G_ROWTILES * H
+            if cut > 0:
+                nc.gpsimd.tensor_tensor(out=t[:, 0:cut], in0=c_sb[j][:, 0:cut], in1=xt_sb[(j, 1)][:, 0:cut], op=ALU.subtract)
+            if cut < R * H:
+                nc.vector.tensor_tensor(out=t[:, cut:], in0=c_sb[j][:, cut:], in1=xt_sb[(j, 1)][:, cut:], op=ALU.subtract)
+            blend[j] = t
+
+        def mm(j):
+            a = apool.tile([P, R, CH], F32, name="at_%d" % j, tag="at")
+            for m in range(4):
+                z = psz.tile([P, CH], F32, name="z", tag="z")
+                cols = slice(m * P, (m + 1) * P)
+                for i in range(3):
+                    nc.tensor.matmul_mx(
+                        out=z[:],
+                        lhsT=w_codes[i][:, cols].bitcast(FP8X4),
+                        lhsT_scale=w_planes[i][:, cols],
+                        rhs=codes[(j, i)][:].bitcast(FP8X4),
+                        rhs_scale=planes[(j, i)][:],
+                        start=(i == 0),
+                        stop=(i == 2),
+                    )
+                nc.scalar.activation(out=a[:, m, :], in_=z[:], func=ACT.Sigmoid, bias=bias[:, m : m + 1], scale=1.0)
+            att_t[j] = a
+
+        def back_jobs(j):
+            jobs = []
+            for r in range(R):
+
+                def job(r=r):
+                    bank = psa.tile([P, H], F32, name="att", tag="att")
+                    for m in range(4):
+                        nc.tensor.transpose(bank[:, m * P : (m + 1) * P], att_t[j][:, m, r * P : (r + 1) * P], ident[:])
+                    part = blend[j][:, r * H : (r + 1) * H]
+                    nc.vector.tensor_tensor(out=part, in0=bank[:], in1=part, op=ALU.mult)
+
+                jobs.append(job)
+            return jobs
+
+        def finish(j, pieces):
+            w = R * H // pieces
+            dram = rows(out, j)
+            for s in range(pieces):
+                cols = slice(s * w, (s + 1) * w)
+                nc.vector.tensor_tensor(out=blend[j][:, cols], in0=blend[j][:, cols], in1=xt_sb[(j, 1)][:, cols], op=ALU.add)
+                nc.sync.dma_start(out=dram[:, cols], in_=blend[j][:, cols])
+
+        for i in range(3):
+            load_w(i)
+            load_x(0, i)
+        load_c(0)
+        for j in range(1, PRELOAD):
+            load_chunk(j)
+        first_jobs = flip_jobs(0)
+        for i in range(3):
+            prep_w(i)
+            first_jobs[2 * i]()
+            first_jobs[2 * i + 1]()
+        bf = const.tile([P, P], F32, name="bf")
+        nc.vector.tensor_copy(out=bf[:], in_=braw[:])
+        bbank = psx.tile([P, 2, 2 * P], F32, name="bbank", tag="xt")
+        nc.tensor.transpose(bbank[:, 0, 0:P], bf[:], ident[:])
+        bias = const.tile([P, 4], F32, name="bias")
+        nc.vector.tensor_copy(out=bias[:], in_=bbank[:, 0, 0:4])
+        for j in range(D_AHEAD):
+            dsub(j)
+
+        for j in range(NCH):
+            mm(j)
+            if j >= 1:
+                finish(j - 1, 1)
+            if j + PRELOAD - 1 < NCH and j >= 1:
+                load_chunk(j + PRELOAD - 1)
+            if j + D_AHEAD < NCH:
+                dsub(j + D_AHEAD)
+            fl = []
+            for jj in TXPLAN.get(j, ()):
+                fl.extend(flip_jobs(jj))
+            bk = back_jobs(j)
+            order = fl[:2]
+            rest = fl[2:]
+            for s in range(max(len(bk), len(rest))):
+                if s < len(bk):
+                    order.append(bk[s])
+                if s < len(rest):
+                    order.append(rest[s])
+            for job in order:
+                job()
+        finish(NCH - 1, 4)

@@ -18,7 +18,7 @@ CH = P * R
 NCH = B // CH
 FLOPS = 2 * B * 3 * K * H
 
-PIN = False
+PIN = True
 G_ROWTILES = 0
 PRELOAD = 4
 D_AHEAD = 2

@@ -19,10 +19,265 @@ NCH = B // CH
 FLOPS = 2 * B * 3 * K * H
 
 PIN = True
-G_ROWTILES = 0
-PRELOAD = 4
-D_AHEAD = 2
-TXPLAN = {0: (1,), 1: (2, 3), 2: (4,), 3: (5,), 4: (6,), 5: (7,)}
+XBUFS, STBUFS, CBUFS, GBUFS, QBUFS, BLBUFS, ABUFS = 3, 6, 4, 2, 3, 5, 3
+PLAN = (
+    ('Lw', 0),
+    ('Lx', 0, 0),
+    ('Lw', 1),
+    ('Lx', 1, 0),
+    ('Lw', 2),
+    ('Lx', 2, 0),
+    ('Lc', 0),
+    ('Lx', 1, 1),
+    ('Lc', 1),
+    ('Lx', 0, 1),
+    ('Lx', 2, 1),
+    ('Lx', 1, 2),
+    ('Lc', 2),
+    ('Lx', 0, 2),
+    ('Lx', 2, 2),
+    ('w', 0, 0, True),
+    ('w', 0, 1, True),
+    ('W', 0),
+    ('x', 0, 0, 0, False),
+    ('x', 0, 1, 0, False),
+    ('q', 0, 0),
+    ('w', 1, 0, True),
+    ('w', 1, 1, True),
+    ('W', 1),
+    ('x', 1, 0, 0, False),
+    ('x', 1, 1, 0, False),
+    ('q', 1, 0),
+    ('w', 2, 0, True),
+    ('w', 2, 1, True),
+    ('W', 2),
+    ('x', 2, 0, 0, False),
+    ('x', 2, 1, 0, False),
+    ('q', 2, 0),
+    ('b',),
+    ('d', 0, 1, 0, False),
+    ('d', 1, 2, 0, False),
+    ('d', 2, 3, 0, False),
+    ('d', 3, 4, 0, False),
+    ('d', 0, 1, 1, False),
+    ('d', 1, 2, 1, False),
+    ('d', 2, 3, 1, False),
+    ('d', 3, 4, 1, False),
+    ('Lx', 1, 3),
+    ('Lc', 3),
+    ('Lx', 0, 3),
+    ('Lx', 2, 3),
+    ('z', 0, 0),
+    ('x', 0, 0, 1, False),
+    ('x', 0, 1, 1, False),
+    ('d', 0, 1, 2, False),
+    ('z', 1, 0),
+    ('x', 1, 0, 1, False),
+    ('q', 0, 1),
+    ('d', 1, 2, 2, False),
+    ('z', 2, 0),
+    ('x', 1, 1, 1, False),
+    ('x', 2, 0, 1, False),
+    ('d', 2, 3, 2, False),
+    ('z', 3, 0),
+    ('q', 1, 1),
+    ('x', 2, 1, 1, False),
+    ('q', 2, 1),
+    ('d', 3, 4, 2, False),
+    ('Lx', 1, 4),
+    ('Lc', 4),
+    ('Lx', 0, 4),
+    ('Lx', 2, 4),
+    ('z', 0, 1),
+    ('a', 0, 0),
+    ('f', 0, 1, 0),
+    ('x', 0, 0, 2, False),
+    ('x', 0, 1, 2, False),
+    ('x', 0, 0, 3, False),
+    ('x', 0, 1, 3, False),
+    ('d', 0, 1, 3, False),
+    ('z', 1, 1),
+    ('a', 1, 0),
+    ('f', 1, 2, 0),
+    ('x', 1, 0, 2, False),
+    ('q', 0, 2),
+    ('x', 1, 0, 3, False),
+    ('q', 0, 3),
+    ('d', 1, 2, 3, False),
+    ('z', 2, 1),
+    ('a', 2, 0),
+    ('f', 2, 3, 0),
+    ('x', 1, 1, 2, False),
+    ('x', 2, 0, 2, False),
+    ('x', 1, 1, 3, False),
+    ('x', 2, 0, 3, False),
+    ('d', 2, 3, 3, False),
+    ('z', 3, 1),
+    ('a', 3, 0),
+    ('f', 3, 4, 0),
+    ('q', 1, 2),
+    ('x', 2, 1, 2, False),
+    ('q', 2, 2),
+    ('q', 1, 3),
+    ('x', 2, 1, 3, False),
+    ('d', 3, 4, 3, False),
+    ('s', 0, 4, 0),
+    ('Lx', 1, 5),
+    ('Lc', 5),
+    ('Lx', 0, 5),
+    ('Lx', 2, 5),
+    ('z', 0, 2),
+    ('a', 0, 1),
+    ('f', 0, 1, 1),
+    ('q', 2, 3),
+    ('x', 0, 0, 4, False),
+    ('x', 0, 1, 4, False),
+    ('d', 0, 1, 4, False),
+    ('z', 1, 2),
+    ('a', 1, 1),
+    ('f', 1, 2, 1),
+    ('x', 1, 0, 4, False),
+    ('q', 0, 4),
+    ('d', 1, 2, 4, False),
+    ('z', 2, 2),
+    ('a', 2, 1),
+    ('f', 2, 3, 1),
+    ('x', 1, 1, 4, False),
+    ('x', 2, 0, 4, False),
+    ('d', 2, 3, 4, False),
+    ('z', 3, 2),
+    ('a', 3, 1),
+    ('f', 3, 4, 1),
+    ('q', 1, 4),
+    ('x', 2, 1, 4, False),
+    ('d', 3, 4, 4, False),
+    ('s', 0, 4, 1),
+    ('Lx', 1, 6),
+    ('Lc', 6),
+    ('Lx', 0, 6),
+    ('Lx', 2, 6),
+    ('z', 0, 3),
+    ('a', 0, 2),
+    ('f', 0, 1, 2),
+    ('q', 2, 4),
+    ('x', 0, 0, 5, False),
+    ('x', 0, 1, 5, False),
+    ('d', 0, 1, 5, False),
+    ('z', 1, 3),
+    ('a', 1, 2),
+    ('f', 1, 2, 2),
+    ('x', 1, 0, 5, False),
+    ('q', 0, 5),
+    ('d', 1, 2, 5, False),
+    ('z', 2, 3),
+    ('a', 2, 2),
+    ('f', 2, 3, 2),
+    ('x', 1, 1, 5, False),
+    ('x', 2, 0, 5, False),
+    ('d', 2, 3, 5, False),
+    ('z', 3, 3),
+    ('a', 3, 2),
+    ('f', 3, 4, 2),
+    ('q', 1, 5),
+    ('x', 2, 1, 5, False),
+    ('d', 3, 4, 5, False),
+    ('s', 0, 4, 2),
+    ('Lx', 1, 7),
+    ('Lc', 7),
+    ('Lx', 0, 7),
+    ('Lx', 2, 7),
+    ('z', 0, 4),
+    ('a', 0, 3),
+    ('f', 0, 1, 3),
+    ('q', 2, 5),
+    ('x', 0, 0, 6, False),
+    ('x', 0, 1, 6, False),
+    ('d', 0, 1, 6, False),
+    ('z', 1, 4),
+    ('a', 1, 3),
+    ('f', 1, 2, 3),
+    ('x', 1, 0, 6, False),
+    ('q', 0, 6),
+    ('d', 1, 2, 6, False),
+    ('z', 2, 4),
+    ('a', 2, 3),
+    ('f', 2, 3, 3),
+    ('x', 1, 1, 6, False),
+    ('x', 2, 0, 6, False),
+    ('d', 2, 3, 6, False),
+    ('z', 3, 4),
+    ('a', 3, 3),
+    ('f', 3, 4, 3),
+    ('q', 1, 6),
+    ('x', 2, 1, 6, False),
+    ('d', 3, 4, 6, False),
+    ('s', 0, 4, 3),
+    ('z', 0, 5),
+    ('a', 0, 4),
+    ('f', 0, 1, 4),
+    ('q', 2, 6),
+    ('x', 0, 0, 7, False),
+    ('x', 0, 1, 7, False),
+    ('d', 0, 1, 7, False),
+    ('z', 1, 5),
+    ('a', 1, 4),
+    ('f', 1, 2, 4),
+    ('x', 1, 0, 7, False),
+    ('q', 0, 7),
+    ('d', 1, 2, 7, False),
+    ('z', 2, 5),
+    ('a', 2, 4),
+    ('f', 2, 3, 4),
+    ('x', 1, 1, 7, False),
+    ('x', 2, 0, 7, False),
+    ('d', 2, 3, 7, False),
+    ('z', 3, 5),
+    ('a', 3, 4),
+    ('f', 3, 4, 4),
+    ('q', 1, 7),
+    ('x', 2, 1, 7, False),
+    ('d', 3, 4, 7, False),
+    ('s', 0, 4, 4),
+    ('z', 0, 6),
+    ('a', 0, 5),
+    ('f', 0, 1, 5),
+    ('q', 2, 7),
+    ('z', 1, 6),
+    ('a', 1, 5),
+    ('f', 1, 2, 5),
+    ('z', 2, 6),
+    ('a', 2, 5),
+    ('f', 2, 3, 5),
+    ('z', 3, 6),
+    ('a', 3, 5),
+    ('f', 3, 4, 5),
+    ('s', 0, 4, 5),
+    ('z', 0, 7),
+    ('a', 0, 6),
+    ('f', 0, 1, 6),
+    ('z', 1, 7),
+    ('a', 1, 6),
+    ('f', 1, 2, 6),
+    ('z', 2, 7),
+    ('a', 2, 6),
+    ('f', 2, 3, 6),
+    ('z', 3, 7),
+    ('a', 3, 6),
+    ('f', 3, 4, 6),
+    ('s', 0, 4, 6),
+    ('a', 0, 7),
+    ('f', 0, 1, 7),
+    ('s', 0, 1, 7),
+    ('a', 1, 7),
+    ('f', 1, 2, 7),
+    ('s', 1, 2, 7),
+    ('a', 2, 7),
+    ('f', 2, 3, 7),
+    ('s', 2, 3, 7),
+    ('a', 3, 7),
+    ('f', 3, 4, 7),
+    ('s', 3, 4, 7),
+)
 
 
 def tile_parentgru_pb_t_kernel(tc, inputs, state, parent_state, c, w_a_w, w_a_b, u_a_w, p_a_w, out):
@@ -33,16 +288,8 @@ def tile_parentgru_pb_t_kernel(tc, inputs, state, parent_state, c, w_a_w, w_a_b,
         if PIN:
             ctx.enter_context(tc.manual_schedule())
         const = ctx.enter_context(tc.tile_pool(name="const", bufs=1))
-        xpool = ctx.enter_context(tc.tile_pool(name="xpool", bufs=3))
-        spool = ctx.enter_context(tc.tile_pool(name="spool", bufs=6))
-        cpool = ctx.enter_context(tc.tile_pool(name="cpool", bufs=4))
-        bpool = ctx.enter_context(tc.tile_pool(name="bpool", bufs=5))
-        gpool = ctx.enter_context(tc.tile_pool(name="gpool", bufs=4))
-        qpool = ctx.enter_context(tc.tile_pool(name="qpool", bufs=3))
-        apool = ctx.enter_context(tc.tile_pool(name="apool", bufs=2))
-        psx = ctx.enter_context(tc.psum_pool(name="psx", bufs=2))
-        psz = ctx.enter_context(tc.psum_pool(name="psz", bufs=4))
-        psa = ctx.enter_context(tc.psum_pool(name="psa", bufs=2))
+        pool = ctx.enter_context(tc.tile_pool(name="pool", bufs=2))
+        psum = ctx.enter_context(tc.psum_pool(name="psum", bufs=8))
 
         ident = const.tile([P, P], F32, name="ident")
         make_identity(nc, ident[:])
@@ -53,181 +300,151 @@ def tile_parentgru_pb_t_kernel(tc, inputs, state, parent_state, c, w_a_w, w_a_b,
         braw = const.tile([P, P], BF16, name="braw")
         nc.vector.memset(braw[:], 0.0)
         nc.scalar.dma_start(out=braw[0:4, :], in_=w_a_b.rearrange("(m p) -> m p", p=P))
+        bias = const.tile([P, 4], F32, name="bias")
 
-        xt_sb = {}
+        x_sb = {}
         c_sb = {}
-        blend = {}
+        grouped = {}
         codes = {}
         planes = {}
-        att_t = {}
-        w_sb = []
-        w_codes = []
-        w_planes = []
+        blend = {}
+        a_t = {}
+        w_sb = {}
+        w_grouped = {}
+        w_codes = {}
+        w_planes = {}
 
         def rows(ap, j):
             return ap[j * CH : (j + 1) * CH, :].rearrange("(p r) k -> p (r k)", r=R)
 
         def load_w(i):
-            t = const.tile([P, R, K], BF16, name="w%d" % i)
-            nc.sync.dma_start(out=t[:], in_=weights[i].rearrange("(m p) k -> p m k", p=P))
-            w_sb.append(t)
+            t = const.tile([P, R * K], BF16, name="w%d" % i)
+            nc.sync.dma_start(out=t[:].rearrange("p (m k) -> p m k", m=R), in_=weights[i].rearrange("(m p) k -> p m k", p=P))
+            w_sb[i] = t
 
         def load_x(j, i):
-            pool = spool if i == 1 else xpool
-            t = pool.tile([P, R * K], BF16, name="x%d_%d" % (i, j), tag="x%d" % i)
+            t = pool.tile([P, R * K], BF16, name="x%d_%d" % (i, j), tag="x%d" % i, bufs=(STBUFS if i == 1 else XBUFS))
             nc.sync.dma_start(out=t[:], in_=rows(acts[i], j))
-            xt_sb[(j, i)] = t
+            x_sb[(j, i)] = t
 
         def load_c(j):
-            t = cpool.tile([P, R * K], BF16, name="c_%d" % j, tag="c")
+            t = pool.tile([P, R * K], BF16, name="c_%d" % j, tag="c", bufs=CBUFS)
             nc.sync.dma_start(out=t[:], in_=rows(c, j))
             c_sb[j] = t
 
-        def load_chunk(j):
-            for i in range(3):
-                load_x(j, i)
-            load_c(j)
-
-        def flip_pair(words, half, g32, on_vector):
-            bank = psx.tile([P, 2, 2 * P], F32, name="bank", tag="xt")
+        def flip_out(g, words, half, on_vector):
+            bank = psum.tile([P, 2, 2 * P], F32, name="bank", tag="bank")
             for rr in range(2):
                 for u in range(2):
                     col = (2 * half + rr) * (K // 2) + u * P
                     nc.tensor.transpose(bank[:, u, rr * P : (rr + 1) * P], words[:, col : col + P], ident[:])
-            dst = g32[:, half * 2 * P : (half + 1) * 2 * P, :]
+            dst = g[:].bitcast(F32).rearrange("q (n u) -> q n u", u=2)[:, half * 2 * P : (half + 1) * 2 * P, :]
             src = bank[:].rearrange("q u n -> q n u")
             if on_vector:
                 nc.vector.tensor_copy(out=dst, in_=src)
             else:
                 nc.scalar.copy(out=dst, in_=src)
 
-        def new_grouped(label):
-            g = gpool.tile([P, 4 * CH], BF16, name="g" + label, tag="g", align_bytes=64)
-            return g, g[:].bitcast(F32).rearrange("q (n u) -> q n u", u=2)
+        def job_w(i, half, on_vector):
+            if half == 0:
+                w_grouped[i] = pool.tile([P, 4 * H], BF16, name="gw%d" % i, tag="gw", bufs=2, align_bytes=64)
+            flip_out(w_grouped[i], w_sb[i][:].bitcast(F32), half, on_vector)
 
-        def quantise(g, cd, pl):
-            nc.vector.quantize_mx(out=cd[:].bitcast(FP8X4), scales=pl[:], in_=g[:])
+        def job_qw(i):
+            w_codes[i] = const.tile([P, H], U32, name="wc%d" % i, align_bytes=64)
+            w_planes[i] = const.tile([P, H], U8, name="wp%d" % i, align_bytes=64)
+            nc.vector.quantize_mx(out=w_codes[i][:].bitcast(FP8X4), scales=w_planes[i][:], in_=w_grouped[i][:])
 
-        def prep_w(i):
-            g, g32 = new_grouped("w%d" % i)
-            words = w_sb[i][:].rearrange("p m k -> p (m k)").bitcast(F32)
-            for half in range(2):
-                flip_pair(words, half, g32, True)
-            cd = const.tile([P, H], U32, name="wc%d" % i, align_bytes=64)
-            pl = const.tile([P, H], U8, name="wp%d" % i, align_bytes=64)
-            quantise(g, cd, pl)
-            w_codes.append(cd)
-            w_planes.append(pl)
+        def job_x(j, i, half, on_vector):
+            if half == 0:
+                grouped[(j, i)] = pool.tile([P, 4 * CH], BF16, name="g%d_%d" % (i, j), tag="g%d" % i, bufs=GBUFS, align_bytes=64)
+            flip_out(grouped[(j, i)], x_sb[(j, i)][:].bitcast(F32), half, on_vector)
 
-        def flip_jobs(j):
-            jobs = []
+        def job_q(j, i):
+            codes[(j, i)] = pool.tile([P, CH], U32, name="xc%d_%d" % (i, j), tag="xc%d" % i, bufs=QBUFS, align_bytes=64)
+            planes[(j, i)] = pool.tile([P, CH], U8, name="xp%d_%d" % (i, j), tag="xp%d" % i, bufs=QBUFS, align_bytes=64)
+            nc.vector.quantize_mx(out=codes[(j, i)][:].bitcast(FP8X4), scales=planes[(j, i)][:], in_=grouped[(j, i)][:])
+
+        def job_d(j, r0, r1, on_gpsimd):
+            if j not in blend:
+                blend[j] = pool.tile([P, R * H], F32, name="bl_%d" % j, tag="bl", bufs=BLBUFS)
+            cols = slice(r0 * H, r1 * H)
+            eng = nc.gpsimd if on_gpsimd else nc.vector
+            eng.tensor_tensor(out=blend[j][:, cols], in0=c_sb[j][:, cols], in1=x_sb[(j, 1)][:, cols], op=ALU.subtract)
+
+        def job_z(j, t):
+            if t == 0:
+                a_t[j] = pool.tile([P, 4, CH], F32, name="a_%d" % j, tag="a", bufs=ABUFS)
+            z = psum.tile([P, CH], F32, name="z", tag="bank")
+            cols = slice(t * P, (t + 1) * P)
             for i in range(3):
-                box = {}
+                nc.tensor.matmul_mx(
+                    out=z[:],
+                    lhsT=w_codes[i][:, cols].bitcast(FP8X4),
+                    lhsT_scale=w_planes[i][:, cols],
+                    rhs=codes[(j, i)][:].bitcast(FP8X4),
+                    rhs_scale=planes[(j, i)][:],
+                    start=(i == 0),
+                    stop=(i == 2),
+                )
+            nc.scalar.activation(out=a_t[j][:, t, :], in_=z[:], func=ACT.Sigmoid, bias=bias[:, t : t + 1], scale=1.0)
 
-                def first(i=i, box=box):
-                    box["g"] = new_grouped("x%d_%d" % (i, j))
-                    flip_pair(xt_sb[(j, i)][:].bitcast(F32), 0, box["g"][1], False)
+        def job_a(j, r):
+            bank = psum.tile([P, H], F32, name="att", tag="bank")
+            for t in range(4):
+                nc.tensor.transpose(bank[:, t * P : (t + 1) * P], a_t[j][:, t, r * P : (r + 1) * P], ident[:])
+            part = blend[j][:, r * H : (r + 1) * H]
+            nc.vector.tensor_tensor(out=part, in0=bank[:], in1=part, op=ALU.mult)
 
-                def second(i=i, box=box):
-                    flip_pair(xt_sb[(j, i)][:].bitcast(F32), 1, box["g"][1], False)
-                    cd = qpool.tile([P, CH], U32, name="xc%d_%d" % (i, j), tag="xc%d" % i, align_bytes=64)
-                    pl = qpool.tile([P, CH], U8, name="xp%d_%d" % (i, j), tag="xp%d" % i, align_bytes=64)
-                    quantise(box["g"][0], cd, pl)
-                    codes[(j, i)] = cd
-                    planes[(j, i)] = pl
+        def job_f(j, r0, r1):
+            cols = slice(r0 * H, r1 * H)
+            nc.vector.tensor_tensor(out=blend[j][:, cols], in0=blend[j][:, cols], in1=x_sb[(j, 1)][:, cols], op=ALU.add)
 
-                jobs.append(first)
-                jobs.append(second)
-            return jobs
+        def job_s(j, r0, r1):
+            cols = slice(r0 * H, r1 * H)
+            nc.sync.dma_start(out=rows(out, j)[:, cols], in_=blend[j][:, cols])
 
-        def dsub(j):
-            t = bpool.tile([P, R * H], F32, name="bl_%d" % j, tag="bl")
-            cut = G_ROWTILES * H
-            if cut > 0:
-                nc.gpsimd.tensor_tensor(out=t[:, 0:cut], in0=c_sb[j][:, 0:cut], in1=xt_sb[(j, 1)][:, 0:cut], op=ALU.subtract)
-            if cut < R * H:
-                nc.vector.tensor_tensor(out=t[:, cut:], in0=c_sb[j][:, cut:], in1=xt_sb[(j, 1)][:, cut:], op=ALU.subtract)
-            blend[j] = t
+        def job_bias():
+            bf = const.tile([P, P], F32, name="bf")
+            nc.vector.tensor_copy(out=bf[:], in_=braw[:])
+            bank = psum.tile([P, 2, 2 * P], F32, name="bbank", tag="bank")
+            nc.tensor.transpose(bank[:, 0, 0:P], bf[:], ident[:])
+            nc.vector.tensor_copy(out=bias[:], in_=bank[:, 0, 0:4])
 
-        def mm(j):
-            a = apool.tile([P, R, CH], F32, name="at_%d" % j, tag="at")
-            for m in range(4):
-                z = psz.tile([P, CH], F32, name="z", tag="z")
-                cols = slice(m * P, (m + 1) * P)
-                for i in range(3):
-                    nc.tensor.matmul_mx(
-                        out=z[:],
-                        lhsT=w_codes[i][:, cols].bitcast(FP8X4),
-                        lhsT_scale=w_planes[i][:, cols],
-                        rhs=codes[(j, i)][:].bitcast(FP8X4),
-                        rhs_scale=planes[(j, i)][:],
-                        start=(i == 0),
-                        stop=(i == 2),
-                    )
-                nc.scalar.activation(out=a[:, m, :], in_=z[:], func=ACT.Sigmoid, bias=bias[:, m : m + 1], scale=1.0)
-            att_t[j] = a
+        def run(job):
+            kind = job[0]
+            if kind == "Lw":
+                load_w(job[1])
+            elif kind == "Lx":
+                load_x(job[2], job[1])
+            elif kind == "Lc":
+                load_c(job[1])
+            elif kind == "w":
+                job_w(job[1], job[2], job[3])
+            elif kind == "W":
+                job_qw(job[1])
+            elif kind == "b":
+                job_bias()
+            elif kind == "x":
+                job_x(job[3], job[1], job[2], job[4])
+            elif kind == "q":
+                job_q(job[2], job[1])
+            elif kind == "d":
+                job_d(job[3], job[1], job[2], job[4])
+            elif kind == "z":
+                job_z(job[2], job[1])
+            elif kind == "a":
+                job_a(job[2], job[1])
+            elif kind == "f":
+                job_f(job[3], job[1], job[2])
+            elif kind == "s":
+                job_s(job[3], job[1], job[2])
+            else:
+                raise ValueError(kind)
 
-        def back_jobs(j):
-            jobs = []
-            for r in range(R):
+        for job in make_plan():
+            run(job)
 
-                def job(r=r):
-                    bank = psa.tile([P, H], F32, name="att", tag="att")
-                    for m in range(4):
-                        nc.tensor.transpose(bank[:, m * P : (m + 1) * P], att_t[j][:, m, r * P : (r + 1) * P], ident[:])
-                    part = blend[j][:, r * H : (r + 1) * H]
-                    nc.vector.tensor_tensor(out=part, in0=bank[:], in1=part, op=ALU.mult)
 
-                jobs.append(job)
-            return jobs
-
-        def finish(j, pieces):
-            w = R * H // pieces
-            dram = rows(out, j)
-            for s in range(pieces):
-                cols = slice(s * w, (s + 1) * w)
-                nc.vector.tensor_tensor(out=blend[j][:, cols], in0=blend[j][:, cols], in1=xt_sb[(j, 1)][:, cols], op=ALU.add)
-                nc.sync.dma_start(out=dram[:, cols], in_=blend[j][:, cols])
-
-        for i in range(3):
-            load_w(i)
-            load_x(0, i)
-        load_c(0)
-        for j in range(1, PRELOAD):
-            load_chunk(j)
-        first_jobs = flip_jobs(0)
-        for i in range(3):
-            prep_w(i)
-            first_jobs[2 * i]()
-            first_jobs[2 * i + 1]()
-        bf = const.tile([P, P], F32, name="bf")
-        nc.vector.tensor_copy(out=bf[:], in_=braw[:])
-        bbank = psx.tile([P, 2, 2 * P], F32, name="bbank", tag="xt")
-        nc.tensor.transpose(bbank[:, 0, 0:P], bf[:], ident[:])
-        bias = const.tile([P, 4], F32, name="bias")
-        nc.vector.tensor_copy(out=bias[:], in_=bbank[:, 0, 0:4])
-        for j in range(D_AHEAD):
-            dsub(j)
-
-        for j in range(NCH):
-            mm(j)
-            if j >= 1:
-                finish(j - 1, 1)
-            if j + PRELOAD - 1 < NCH and j >= 1:
-                load_chunk(j + PRELOAD - 1)
-            if j + D_AHEAD < NCH:
-                dsub(j + D_AHEAD)
-            fl = []
-            for jj in TXPLAN.get(j, ()):
-                fl.extend(flip_jobs(jj))
-            bk = back_jobs(j)
-            order = fl[:2]
-            rest = fl[2:]
-            for s in range(max(len(bk), len(rest))):
-                if s < len(bk):
-                    order.append(bk[s])
-                if s < len(rest):
-                    order.append(rest[s])
-            for job in order:
-                job()
-        finish(NCH - 1, 4)
+def make_plan():
+    return PLAN

@@ -13,9 +13,7 @@ ALU = mybir.AluOpType
 
 P = 128
 B, K, H = 4096, 512, 512
-R = 4
-CH = P * R
-NCH = B // CH
+SIZES = (2, 2, 2, 2, 4, 4, 4, 4, 4, 2, 2)
 FLOPS = 2 * B * 3 * K * H
 
 PIN = True
@@ -36,247 +34,270 @@ PLAN = (
     ('Lc', 2),
     ('Lx', 0, 2),
     ('Lx', 2, 2),
+    ('b',),
     ('w', 0, 0, True),
     ('w', 0, 1, True),
     ('W', 0),
     ('x', 0, 0, 0, False),
-    ('x', 0, 1, 0, False),
     ('q', 0, 0),
     ('w', 1, 0, True),
     ('w', 1, 1, True),
     ('W', 1),
     ('x', 1, 0, 0, False),
-    ('x', 1, 1, 0, False),
     ('q', 1, 0),
     ('w', 2, 0, True),
     ('w', 2, 1, True),
     ('W', 2),
     ('x', 2, 0, 0, False),
-    ('x', 2, 1, 0, False),
     ('q', 2, 0),
-    ('b',),
+    ('x', 0, 0, 1, False),
+    ('x', 1, 0, 1, False),
+    ('q', 0, 1),
+    ('x', 2, 0, 1, False),
+    ('q', 1, 1),
+    ('q', 2, 1),
     ('d', 0, 1, 0, False),
     ('d', 1, 2, 0, False),
-    ('d', 2, 3, 0, False),
-    ('d', 3, 4, 0, False),
     ('d', 0, 1, 1, False),
     ('d', 1, 2, 1, False),
-    ('d', 2, 3, 1, False),
-    ('d', 3, 4, 1, False),
     ('Lx', 1, 3),
     ('Lc', 3),
     ('Lx', 0, 3),
     ('Lx', 2, 3),
-    ('z', 0, 0),
-    ('x', 0, 0, 1, False),
-    ('x', 0, 1, 1, False),
     ('d', 0, 1, 2, False),
-    ('z', 1, 0),
-    ('x', 1, 0, 1, False),
-    ('q', 0, 1),
+    ('z', 0, 0),
+    ('x', 0, 0, 2, False),
     ('d', 1, 2, 2, False),
-    ('z', 2, 0),
-    ('x', 1, 1, 1, False),
-    ('x', 2, 0, 1, False),
-    ('d', 2, 3, 2, False),
-    ('z', 3, 0),
-    ('q', 1, 1),
-    ('x', 2, 1, 1, False),
-    ('q', 2, 1),
-    ('d', 3, 4, 2, False),
+    ('z', 1, 0),
+    ('x', 1, 0, 2, False),
+    ('q', 0, 2),
+    ('x', 2, 0, 2, False),
+    ('q', 1, 2),
     ('Lx', 1, 4),
     ('Lc', 4),
     ('Lx', 0, 4),
     ('Lx', 2, 4),
-    ('z', 0, 1),
-    ('a', 0, 0),
-    ('f', 0, 1, 0),
-    ('x', 0, 0, 2, False),
-    ('x', 0, 1, 2, False),
-    ('x', 0, 0, 3, False),
-    ('x', 0, 1, 3, False),
     ('d', 0, 1, 3, False),
+    ('z', 0, 1),
+    ('q', 2, 2),
+    ('a', 0, 0),
+    ('x', 0, 0, 3, False),
+    ('d', 1, 2, 3, False),
     ('z', 1, 1),
     ('a', 1, 0),
-    ('f', 1, 2, 0),
-    ('x', 1, 0, 2, False),
-    ('q', 0, 2),
     ('x', 1, 0, 3, False),
     ('q', 0, 3),
-    ('d', 1, 2, 3, False),
-    ('z', 2, 1),
-    ('a', 2, 0),
-    ('f', 2, 3, 0),
-    ('x', 1, 1, 2, False),
-    ('x', 2, 0, 2, False),
-    ('x', 1, 1, 3, False),
+    ('f', 0, 1, 0),
     ('x', 2, 0, 3, False),
-    ('d', 2, 3, 3, False),
-    ('z', 3, 1),
-    ('a', 3, 0),
-    ('f', 3, 4, 0),
-    ('q', 1, 2),
-    ('x', 2, 1, 2, False),
-    ('q', 2, 2),
     ('q', 1, 3),
-    ('x', 2, 1, 3, False),
-    ('d', 3, 4, 3, False),
-    ('s', 0, 4, 0),
     ('Lx', 1, 5),
     ('Lc', 5),
     ('Lx', 0, 5),
     ('Lx', 2, 5),
-    ('z', 0, 2),
-    ('a', 0, 1),
-    ('f', 0, 1, 1),
-    ('q', 2, 3),
-    ('x', 0, 0, 4, False),
-    ('x', 0, 1, 4, False),
     ('d', 0, 1, 4, False),
-    ('z', 1, 2),
-    ('a', 1, 1),
-    ('f', 1, 2, 1),
+    ('d', 1, 2, 4, False),
+    ('z', 0, 2),
+    ('q', 2, 3),
+    ('a', 0, 1),
+    ('x', 0, 0, 4, False),
+    ('f', 1, 2, 0),
+    ('s', 0, 2, 0),
+    ('x', 0, 1, 4, False),
     ('x', 1, 0, 4, False),
     ('q', 0, 4),
-    ('d', 1, 2, 4, False),
-    ('z', 2, 2),
-    ('a', 2, 1),
-    ('f', 2, 3, 1),
-    ('x', 1, 1, 4, False),
-    ('x', 2, 0, 4, False),
     ('d', 2, 3, 4, False),
-    ('z', 3, 2),
-    ('a', 3, 1),
-    ('f', 3, 4, 1),
+    ('d', 3, 4, 4, False),
+    ('z', 1, 2),
+    ('a', 1, 1),
+    ('x', 1, 1, 4, False),
+    ('f', 0, 1, 1),
+    ('x', 2, 0, 4, False),
     ('q', 1, 4),
     ('x', 2, 1, 4, False),
-    ('d', 3, 4, 4, False),
-    ('s', 0, 4, 1),
     ('Lx', 1, 6),
     ('Lc', 6),
     ('Lx', 0, 6),
     ('Lx', 2, 6),
-    ('z', 0, 3),
-    ('a', 0, 2),
-    ('f', 0, 1, 2),
-    ('q', 2, 4),
-    ('x', 0, 0, 5, False),
-    ('x', 0, 1, 5, False),
     ('d', 0, 1, 5, False),
-    ('z', 1, 3),
-    ('a', 1, 2),
-    ('f', 1, 2, 2),
+    ('d', 1, 2, 5, False),
+    ('z', 0, 3),
+    ('q', 2, 4),
+    ('a', 0, 2),
+    ('x', 0, 0, 5, False),
+    ('f', 1, 2, 1),
+    ('s', 0, 2, 1),
+    ('x', 0, 1, 5, False),
     ('x', 1, 0, 5, False),
     ('q', 0, 5),
-    ('d', 1, 2, 5, False),
-    ('z', 2, 3),
-    ('a', 2, 2),
-    ('f', 2, 3, 2),
-    ('x', 1, 1, 5, False),
-    ('x', 2, 0, 5, False),
     ('d', 2, 3, 5, False),
-    ('z', 3, 3),
-    ('a', 3, 2),
-    ('f', 3, 4, 2),
+    ('d', 3, 4, 5, False),
+    ('z', 1, 3),
+    ('a', 1, 2),
+    ('x', 1, 1, 5, False),
+    ('f', 0, 1, 2),
+    ('x', 2, 0, 5, False),
     ('q', 1, 5),
     ('x', 2, 1, 5, False),
-    ('d', 3, 4, 5, False),
-    ('s', 0, 4, 2),
     ('Lx', 1, 7),
     ('Lc', 7),
     ('Lx', 0, 7),
     ('Lx', 2, 7),
+    ('d', 0, 1, 6, False),
     ('z', 0, 4),
-    ('a', 0, 3),
-    ('f', 0, 1, 3),
     ('q', 2, 5),
     ('x', 0, 0, 6, False),
-    ('x', 0, 1, 6, False),
-    ('d', 0, 1, 6, False),
+    ('d', 1, 2, 6, False),
     ('z', 1, 4),
-    ('a', 1, 3),
-    ('f', 1, 2, 3),
+    ('a', 0, 3),
+    ('x', 0, 1, 6, False),
+    ('f', 1, 2, 2),
+    ('s', 0, 2, 2),
     ('x', 1, 0, 6, False),
     ('q', 0, 6),
-    ('d', 1, 2, 6, False),
-    ('z', 2, 4),
-    ('a', 2, 3),
-    ('f', 2, 3, 3),
-    ('x', 1, 1, 6, False),
-    ('x', 2, 0, 6, False),
     ('d', 2, 3, 6, False),
-    ('z', 3, 4),
-    ('a', 3, 3),
-    ('f', 3, 4, 3),
-    ('q', 1, 6),
-    ('x', 2, 1, 6, False),
+    ('z', 2, 4),
+    ('x', 1, 1, 6, False),
     ('d', 3, 4, 6, False),
-    ('s', 0, 4, 3),
-    ('z', 0, 5),
-    ('a', 0, 4),
-    ('f', 0, 1, 4),
-    ('q', 2, 6),
-    ('x', 0, 0, 7, False),
-    ('x', 0, 1, 7, False),
+    ('z', 3, 4),
+    ('a', 1, 3),
+    ('x', 2, 0, 6, False),
+    ('q', 1, 6),
+    ('f', 0, 1, 3),
+    ('x', 2, 1, 6, False),
+    ('Lx', 1, 8),
+    ('Lc', 8),
+    ('Lx', 0, 8),
+    ('Lx', 2, 8),
     ('d', 0, 1, 7, False),
+    ('z', 0, 5),
+    ('q', 2, 6),
+    ('a', 0, 4),
+    ('x', 0, 0, 7, False),
+    ('f', 1, 2, 3),
+    ('s', 0, 2, 3),
+    ('d', 1, 2, 7, False),
     ('z', 1, 5),
     ('a', 1, 4),
-    ('f', 1, 2, 4),
+    ('x', 0, 1, 7, False),
+    ('f', 0, 1, 4),
     ('x', 1, 0, 7, False),
     ('q', 0, 7),
-    ('d', 1, 2, 7, False),
+    ('d', 2, 3, 7, False),
     ('z', 2, 5),
     ('a', 2, 4),
-    ('f', 2, 3, 4),
     ('x', 1, 1, 7, False),
-    ('x', 2, 0, 7, False),
-    ('d', 2, 3, 7, False),
+    ('f', 1, 2, 4),
+    ('d', 3, 4, 7, False),
     ('z', 3, 5),
     ('a', 3, 4),
-    ('f', 3, 4, 4),
+    ('x', 2, 0, 7, False),
     ('q', 1, 7),
+    ('f', 2, 3, 4),
     ('x', 2, 1, 7, False),
-    ('d', 3, 4, 7, False),
-    ('s', 0, 4, 4),
+    ('Lx', 1, 9),
+    ('Lc', 9),
+    ('Lx', 0, 9),
+    ('Lx', 2, 9),
+    ('d', 0, 1, 8, False),
     ('z', 0, 6),
-    ('a', 0, 5),
-    ('f', 0, 1, 5),
     ('q', 2, 7),
+    ('a', 0, 5),
+    ('x', 0, 0, 8, False),
+    ('f', 3, 4, 4),
+    ('s', 0, 4, 4),
+    ('d', 1, 2, 8, False),
     ('z', 1, 6),
     ('a', 1, 5),
-    ('f', 1, 2, 5),
+    ('x', 0, 1, 8, False),
+    ('f', 0, 1, 5),
+    ('x', 1, 0, 8, False),
+    ('q', 0, 8),
+    ('d', 2, 3, 8, False),
     ('z', 2, 6),
     ('a', 2, 5),
-    ('f', 2, 3, 5),
+    ('x', 1, 1, 8, False),
+    ('f', 1, 2, 5),
+    ('d', 3, 4, 8, False),
     ('z', 3, 6),
     ('a', 3, 5),
+    ('x', 2, 0, 8, False),
+    ('q', 1, 8),
+    ('f', 2, 3, 5),
+    ('x', 2, 1, 8, False),
+    ('Lx', 1, 10),
+    ('Lc', 10),
+    ('Lx', 0, 10),
+    ('Lx', 2, 10),
+    ('z', 0, 7),
+    ('q', 2, 8),
+    ('a', 0, 6),
     ('f', 3, 4, 5),
     ('s', 0, 4, 5),
-    ('z', 0, 7),
-    ('a', 0, 6),
-    ('f', 0, 1, 6),
+    ('d', 0, 1, 9, False),
     ('z', 1, 7),
     ('a', 1, 6),
-    ('f', 1, 2, 6),
+    ('x', 0, 0, 9, False),
+    ('f', 0, 1, 6),
     ('z', 2, 7),
     ('a', 2, 6),
-    ('f', 2, 3, 6),
+    ('x', 1, 0, 9, False),
+    ('q', 0, 9),
+    ('f', 1, 2, 6),
+    ('d', 1, 2, 9, False),
     ('z', 3, 7),
     ('a', 3, 6),
+    ('x', 2, 0, 9, False),
+    ('q', 1, 9),
+    ('f', 2, 3, 6),
+    ('z', 0, 8),
+    ('q', 2, 9),
+    ('a', 0, 7),
     ('f', 3, 4, 6),
     ('s', 0, 4, 6),
-    ('a', 0, 7),
-    ('f', 0, 1, 7),
-    ('s', 0, 1, 7),
+    ('d', 0, 1, 10, False),
+    ('z', 1, 8),
     ('a', 1, 7),
-    ('f', 1, 2, 7),
-    ('s', 1, 2, 7),
+    ('x', 0, 0, 10, False),
+    ('f', 0, 1, 7),
+    ('z', 2, 8),
     ('a', 2, 7),
-    ('f', 2, 3, 7),
-    ('s', 2, 3, 7),
+    ('x', 1, 0, 10, False),
+    ('q', 0, 10),
+    ('f', 1, 2, 7),
+    ('d', 1, 2, 10, False),
+    ('z', 3, 8),
     ('a', 3, 7),
+    ('x', 2, 0, 10, False),
+    ('q', 1, 10),
+    ('f', 2, 3, 7),
+    ('z', 0, 9),
+    ('q', 2, 10),
+    ('a', 0, 8),
     ('f', 3, 4, 7),
-    ('s', 3, 4, 7),
+    ('s', 0, 4, 7),
+    ('a', 1, 8),
+    ('f', 0, 1, 8),
+    ('z', 1, 9),
+    ('a', 2, 8),
+    ('f', 1, 2, 8),
+    ('a', 3, 8),
+    ('f', 2, 3, 8),
+    ('z', 0, 10),
+    ('a', 0, 9),
+    ('f', 3, 4, 8),
+    ('s', 0, 4, 8),
+    ('z', 1, 10),
+    ('a', 1, 9),
+    ('f', 0, 1, 9),
+    ('s', 0, 1, 9),
+    ('a', 0, 10),
+    ('f', 1, 2, 9),
+    ('s', 1, 2, 9),
+    ('a', 1, 10),
+    ('f', 0, 1, 10),
+    ('s', 0, 1, 10),
+    ('f', 1, 2, 10),
+    ('s', 1, 2, 10),
 )
 
 
@@ -314,32 +335,34 @@ def tile_parentgru_pb_t_kernel(tc, inputs, state, parent_state, c, w_a_w, w_a_b,
         w_codes = {}
         w_planes = {}
 
+        first_row = [P * sum(SIZES[:j]) for j in range(len(SIZES))]
+
         def rows(ap, j):
-            return ap[j * CH : (j + 1) * CH, :].rearrange("(p r) k -> p (r k)", r=R)
+            return ap[first_row[j] : first_row[j] + P * SIZES[j], :].rearrange("(p r) k -> p (r k)", r=SIZES[j])
 
         def load_w(i):
-            t = const.tile([P, R * K], BF16, name="w%d" % i)
-            nc.sync.dma_start(out=t[:].rearrange("p (m k) -> p m k", m=R), in_=weights[i].rearrange("(m p) k -> p m k", p=P))
+            t = const.tile([P, 4 * K], BF16, name="w%d" % i)
+            nc.sync.dma_start(out=t[:].rearrange("p (m k) -> p m k", m=4), in_=weights[i].rearrange("(m p) k -> p m k", p=P))
             w_sb[i] = t
 
         def load_x(j, i):
-            t = pool.tile([P, R * K], BF16, name="x%d_%d" % (i, j), tag="x%d" % i, bufs=(STBUFS if i == 1 else XBUFS))
+            t = pool.tile([P, SIZES[j] * K], BF16, name="x%d_%d" % (i, j), tag="x%d" % i, bufs=(STBUFS if i == 1 else XBUFS))
             nc.sync.dma_start(out=t[:], in_=rows(acts[i], j))
             x_sb[(j, i)] = t
 
         def load_c(j):
-            t = pool.tile([P, R * K], BF16, name="c_%d" % j, tag="c", bufs=CBUFS)
+            t = pool.tile([P, SIZES[j] * K], BF16, name="c_%d" % j, tag="c", bufs=CBUFS)
             nc.sync.dma_start(out=t[:], in_=rows(c, j))
             c_sb[j] = t
 
-        def flip_out(g, words, half, on_vector):
+        def flip_out(g, words, half, on_vector, tiles):
             bank = psum.tile([P, 2, 2 * P], F32, name="bank", tag="bank")
-            for rr in range(2):
+            for rr in range(tiles):
                 for u in range(2):
                     col = (2 * half + rr) * (K // 2) + u * P
                     nc.tensor.transpose(bank[:, u, rr * P : (rr + 1) * P], words[:, col : col + P], ident[:])
-            dst = g[:].bitcast(F32).rearrange("q (n u) -> q n u", u=2)[:, half * 2 * P : (half + 1) * 2 * P, :]
-            src = bank[:].rearrange("q u n -> q n u")
+            dst = g[:].bitcast(F32).rearrange("q (n u) -> q n u", u=2)[:, half * 2 * P : half * 2 * P + tiles * P, :]
+            src = bank[:, :, 0 : tiles * P].rearrange("q u n -> q n u")
             if on_vector:
                 nc.vector.tensor_copy(out=dst, in_=src)
             else:
@@ -348,7 +371,7 @@ def tile_parentgru_pb_t_kernel(tc, inputs, state, parent_state, c, w_a_w, w_a_b,
         def job_w(i, half, on_vector):
             if half == 0:
                 w_grouped[i] = pool.tile([P, 4 * H], BF16, name="gw%d" % i, tag="gw", bufs=2, align_bytes=64)
-            flip_out(w_grouped[i], w_sb[i][:].bitcast(F32), half, on_vector)
+            flip_out(w_grouped[i], w_sb[i][:].bitcast(F32), half, on_vector, 2)
 
         def job_qw(i):
             w_codes[i] = const.tile([P, H], U32, name="wc%d" % i, align_bytes=64)
@@ -357,37 +380,45 @@ def tile_parentgru_pb_t_kernel(tc, inputs, state, parent_state, c, w_a_w, w_a_b,
 
         def job_x(j, i, half, on_vector):
             if half == 0:
-                grouped[(j, i)] = pool.tile([P, 4 * CH], BF16, name="g%d_%d" % (i, j), tag="g%d" % i, bufs=GBUFS, align_bytes=64)
-            flip_out(grouped[(j, i)], x_sb[(j, i)][:].bitcast(F32), half, on_vector)
+                grouped[(j, i)] = pool.tile([P, 4 * P * SIZES[j]], BF16, name="g%d_%d" % (i, j), tag="g%d" % i, bufs=GBUFS, align_bytes=64)
+            flip_out(grouped[(j, i)], x_sb[(j, i)][:].bitcast(F32), half, on_vector, min(2, SIZES[j] - 2 * half))
 
         def job_q(j, i):
-            codes[(j, i)] = pool.tile([P, CH], U32, name="xc%d_%d" % (i, j), tag="xc%d" % i, bufs=QBUFS, align_bytes=64)
-            planes[(j, i)] = pool.tile([P, CH], U8, name="xp%d_%d" % (i, j), tag="xp%d" % i, bufs=QBUFS, align_bytes=64)
+            codes[(j, i)] = pool.tile([P, P * SIZES[j]], U32, name="xc%d_%d" % (i, j), tag="xc%d" % i, bufs=QBUFS, align_bytes=64)
+            planes[(j, i)] = pool.tile([P, P * SIZES[j]], U8, name="xp%d_%d" % (i, j), tag="xp%d" % i, bufs=QBUFS, align_bytes=64)
             nc.vector.quantize_mx(out=codes[(j, i)][:].bitcast(FP8X4), scales=planes[(j, i)][:], in_=grouped[(j, i)][:])
 
         def job_d(j, r0, r1, on_gpsimd):
             if j not in blend:
-                blend[j] = pool.tile([P, R * H], F32, name="bl_%d" % j, tag="bl", bufs=BLBUFS)
+                blend[j] = pool.tile([P, SIZES[j] * H], F32, name="bl_%d" % j, tag="bl", bufs=BLBUFS)
             cols = slice(r0 * H, r1 * H)
             eng = nc.gpsimd if on_gpsimd else nc.vector
             eng.tensor_tensor(out=blend[j][:, cols], in0=c_sb[j][:, cols], in1=x_sb[(j, 1)][:, cols], op=ALU.subtract)
 
-        def job_z(j, t):
-            if t == 0:
-                a_t[j] = pool.tile([P, 4, CH], F32, name="a_%d" % j, tag="a", bufs=ABUFS)
-            z = psum.tile([P, CH], F32, name="z", tag="bank")
-            cols = slice(t * P, (t + 1) * P)
-            for i in range(3):
-                nc.tensor.matmul_mx(
-                    out=z[:],
-                    lhsT=w_codes[i][:, cols].bitcast(FP8X4),
-                    lhsT_scale=w_planes[i][:, cols],
-                    rhs=codes[(j, i)][:].bitcast(FP8X4),
-                    rhs_scale=planes[(j, i)][:],
-                    start=(i == 0),
-                    stop=(i == 2),
+        def job_z(j, k):
+            n = P * SIZES[j]
+            per_bank = 4 // SIZES[j]
+            if k == 0:
+                a_t[j] = pool.tile([P, 4, n], F32, name="a_%d" % j, tag="a", bufs=ABUFS)
+            z = psum.tile([P, 4 * P], F32, name="z", tag="bank")
+            for s in range(per_bank):
+                t = k * per_bank + s
+                cols = slice(t * P, (t + 1) * P)
+                for i in range(3):
+                    nc.tensor.matmul_mx(
+                        out=z[:, s * n : (s + 1) * n],
+                        lhsT=w_codes[i][:, cols].bitcast(FP8X4),
+                        lhsT_scale=w_planes[i][:, cols],
+                        rhs=codes[(j, i)][:].bitcast(FP8X4),
+                        rhs_scale=planes[(j, i)][:],
+                        start=(i == 0),
+                        stop=(i == 2),
+                    )
+            for s in range(per_bank):
+                t = k * per_bank + s
+                nc.scalar.activation(
+                    out=a_t[j][:, t, :], in_=z[:, s * n : (s + 1) * n], func=ACT.Sigmoid, bias=bias[:, t : t + 1], scale=1.0
                 )
-            nc.scalar.activation(out=a_t[j][:, t, :], in_=z[:], func=ACT.Sigmoid, bias=bias[:, t : t + 1], scale=1.0)
 
         def job_a(j, r):
             bank = psum.tile([P, H], F32, name="att", tag="bank")

@@ -20,10 +20,10 @@ PIN = True
 XBUFS, STBUFS, CBUFS, GBUFS, QBUFS, BLBUFS, ABUFS = 3, 6, 4, 2, 3, 5, 3
 PLAN = (
     ('Lw', 0),
-    ('Lx', 0, 0),
     ('Lw', 1),
-    ('Lx', 1, 0),
     ('Lw', 2),
+    ('Lx', 0, 0),
+    ('Lx', 1, 0),
     ('Lx', 2, 0),
     ('Lc', 0),
     ('Lx', 1, 1),
@@ -35,19 +35,19 @@ PLAN = (
     ('Lx', 0, 2),
     ('Lx', 2, 2),
     ('b',),
-    ('w', 0, 0, True),
+    ('w', 0, 0, False),
     ('w', 0, 1, True),
     ('W', 0),
-    ('x', 0, 0, 0, False),
-    ('q', 0, 0),
-    ('w', 1, 0, True),
+    ('w', 1, 0, False),
     ('w', 1, 1, True),
     ('W', 1),
-    ('x', 1, 0, 0, False),
-    ('q', 1, 0),
-    ('w', 2, 0, True),
+    ('w', 2, 0, False),
     ('w', 2, 1, True),
     ('W', 2),
+    ('x', 0, 0, 0, False),
+    ('q', 0, 0),
+    ('x', 1, 0, 0, False),
+    ('q', 1, 0),
     ('x', 2, 0, 0, False),
     ('q', 2, 0),
     ('x', 0, 0, 1, False),
@@ -320,7 +320,7 @@ def tile_parentgru_pb_t_kernel(tc, inputs, state, parent_state, c, w_a_w, w_a_b,
         nc.scalar.activation(out=warmed[:], in_=warm[:], func=ACT.Sigmoid)
         braw = const.tile([P, P], BF16, name="braw")
         nc.vector.memset(braw[:], 0.0)
-        nc.scalar.dma_start(out=braw[0:4, :], in_=w_a_b.rearrange("(m p) -> m p", p=P))
+        nc.sync.dma_start(out=braw[0:4, :], in_=w_a_b.rearrange("(m p) -> m p", p=P))
         bias = const.tile([P, 4], F32, name="bias")
 
         x_sb = {}

@@ -56,18 +56,15 @@ PLAN = (
     ('x', 2, 0, 1, False),
     ('q', 1, 1),
     ('q', 2, 1),
-    ('d', 0, 1, 0, False),
-    ('d', 1, 2, 0, False),
-    ('d', 0, 1, 1, False),
-    ('d', 1, 2, 1, False),
+    ('d', 0, 2, 0, False),
+    ('d', 0, 2, 1, False),
     ('Lx', 1, 3),
     ('Lc', 3),
     ('Lx', 0, 3),
     ('Lx', 2, 3),
-    ('d', 0, 1, 2, False),
+    ('d', 0, 2, 2, False),
     ('z', 0, 0),
     ('x', 0, 0, 2, False),
-    ('d', 1, 2, 2, False),
     ('z', 1, 0),
     ('x', 1, 0, 2, False),
     ('q', 0, 2),
@@ -77,12 +74,11 @@ PLAN = (
     ('Lc', 4),
     ('Lx', 0, 4),
     ('Lx', 2, 4),
-    ('d', 0, 1, 3, False),
+    ('d', 0, 2, 3, False),
     ('z', 0, 1),
     ('q', 2, 2),
     ('a', 0, 0),
     ('x', 0, 0, 3, False),
-    ('d', 1, 2, 3, False),
     ('z', 1, 1),
     ('a', 1, 0),
     ('x', 1, 0, 3, False),
@@ -94,8 +90,7 @@ PLAN = (
     ('Lc', 5),
     ('Lx', 0, 5),
     ('Lx', 2, 5),
-    ('d', 0, 1, 4, False),
-    ('d', 1, 2, 4, False),
+    ('d', 0, 2, 4, False),
     ('z', 0, 2),
     ('q', 2, 3),
     ('a', 0, 1),
@@ -106,7 +101,7 @@ PLAN = (
     ('x', 1, 0, 4, False),
     ('q', 0, 4),
     ('d', 2, 3, 4, False),
-    ('d', 3, 4, 4, False),
+    ('e', 3, 4),
     ('z', 1, 2),
     ('a', 1, 1),
     ('x', 1, 1, 4, False),
@@ -118,8 +113,7 @@ PLAN = (
     ('Lc', 6),
     ('Lx', 0, 6),
     ('Lx', 2, 6),
-    ('d', 0, 1, 5, False),
-    ('d', 1, 2, 5, False),
+    ('d', 0, 2, 5, False),
     ('z', 0, 3),
     ('q', 2, 4),
     ('a', 0, 2),
@@ -130,7 +124,7 @@ PLAN = (
     ('x', 1, 0, 5, False),
     ('q', 0, 5),
     ('d', 2, 3, 5, False),
-    ('d', 3, 4, 5, False),
+    ('e', 3, 5),
     ('z', 1, 3),
     ('a', 1, 2),
     ('x', 1, 1, 5, False),
@@ -142,11 +136,10 @@ PLAN = (
     ('Lc', 7),
     ('Lx', 0, 7),
     ('Lx', 2, 7),
-    ('d', 0, 1, 6, False),
+    ('d', 0, 2, 6, False),
     ('z', 0, 4),
     ('q', 2, 5),
     ('x', 0, 0, 6, False),
-    ('d', 1, 2, 6, False),
     ('z', 1, 4),
     ('a', 0, 3),
     ('x', 0, 1, 6, False),
@@ -157,7 +150,7 @@ PLAN = (
     ('d', 2, 3, 6, False),
     ('z', 2, 4),
     ('x', 1, 1, 6, False),
-    ('d', 3, 4, 6, False),
+    ('e', 3, 6),
     ('z', 3, 4),
     ('a', 1, 3),
     ('x', 2, 0, 6, False),
@@ -168,14 +161,13 @@ PLAN = (
     ('Lc', 8),
     ('Lx', 0, 8),
     ('Lx', 2, 8),
-    ('d', 0, 1, 7, False),
+    ('d', 0, 2, 7, False),
     ('z', 0, 5),
     ('q', 2, 6),
     ('a', 0, 4),
     ('x', 0, 0, 7, False),
     ('f', 1, 2, 3),
     ('s', 0, 2, 3),
-    ('d', 1, 2, 7, False),
     ('z', 1, 5),
     ('a', 1, 4),
     ('x', 0, 1, 7, False),
@@ -187,7 +179,7 @@ PLAN = (
     ('a', 2, 4),
     ('x', 1, 1, 7, False),
     ('f', 1, 2, 4),
-    ('d', 3, 4, 7, False),
+    ('e', 3, 7),
     ('z', 3, 5),
     ('a', 3, 4),
     ('x', 2, 0, 7, False),
@@ -198,14 +190,13 @@ PLAN = (
     ('Lc', 9),
     ('Lx', 0, 9),
     ('Lx', 2, 9),
-    ('d', 0, 1, 8, False),
+    ('d', 0, 2, 8, False),
     ('z', 0, 6),
     ('q', 2, 7),
     ('a', 0, 5),
     ('x', 0, 0, 8, False),
     ('f', 3, 4, 4),
     ('s', 0, 4, 4),
-    ('d', 1, 2, 8, False),
     ('z', 1, 6),
     ('a', 1, 5),
     ('x', 0, 1, 8, False),
@@ -217,7 +208,7 @@ PLAN = (
     ('a', 2, 5),
     ('x', 1, 1, 8, False),
     ('f', 1, 2, 5),
-    ('d', 3, 4, 8, False),
+    ('e', 3, 8),
     ('z', 3, 6),
     ('a', 3, 5),
     ('x', 2, 0, 8, False),
@@ -233,7 +224,7 @@ PLAN = (
     ('a', 0, 6),
     ('f', 3, 4, 5),
     ('s', 0, 4, 5),
-    ('d', 0, 1, 9, False),
+    ('d', 0, 2, 9, False),
     ('z', 1, 7),
     ('a', 1, 6),
     ('x', 0, 0, 9, False),
@@ -243,7 +234,6 @@ PLAN = (
     ('x', 1, 0, 9, False),
     ('q', 0, 9),
     ('f', 1, 2, 6),
-    ('d', 1, 2, 9, False),
     ('z', 3, 7),
     ('a', 3, 6),
     ('x', 2, 0, 9, False),
@@ -254,7 +244,7 @@ PLAN = (
     ('a', 0, 7),
     ('f', 3, 4, 6),
     ('s', 0, 4, 6),
-    ('d', 0, 1, 10, False),
+    ('d', 0, 2, 10, False),
     ('z', 1, 8),
     ('a', 1, 7),
     ('x', 0, 0, 10, False),
@@ -264,7 +254,6 @@ PLAN = (
     ('x', 1, 0, 10, False),
     ('q', 0, 10),
     ('f', 1, 2, 7),
-    ('d', 1, 2, 10, False),
     ('z', 3, 8),
     ('a', 3, 7),
     ('x', 2, 0, 10, False),
@@ -323,6 +312,10 @@ def tile_parentgru_pb_t_kernel(tc, inputs, state, parent_state, c, w_a_w, w_a_b,
         nc.sync.dma_start(out=braw[0:4, :], in_=w_a_b.rearrange("(m p) -> m p", p=P))
         bias = const.tile([P, 4], F32, name="bias")
 
+        ident_bf = const.tile([P, P], BF16, name="ident_bf")
+        nc.vector.tensor_copy(out=ident_bf[:], in_=ident[:])
+        neg_ident_bf = const.tile([P, P], BF16, name="neg_ident_bf")
+        nc.vector.tensor_scalar_mul(out=neg_ident_bf[:], in0=ident[:], scalar1=-1.0)
         x_sb = {}
         c_sb = {}
         grouped = {}
@@ -394,6 +387,15 @@ def tile_parentgru_pb_t_kernel(tc, inputs, state, parent_state, c, w_a_w, w_a_b,
             cols = slice(r0 * H, r1 * H)
             eng = nc.gpsimd if on_gpsimd else nc.vector
             eng.tensor_tensor(out=blend[j][:, cols], in0=c_sb[j][:, cols], in1=x_sb[(j, 1)][:, cols], op=ALU.subtract)
+
+        def job_e(j, r):
+            if j not in blend:
+                blend[j] = pool.tile([P, SIZES[j] * H], F32, name="bl_%d" % j, tag="bl", bufs=BLBUFS)
+            cols = slice(r * H, (r + 1) * H)
+            bank = psum.tile([P, H], F32, name="dbank", tag="bank")
+            nc.tensor.matmul(bank[:], lhsT=ident_bf[:], rhs=c_sb[j][:, cols], start=True, stop=False)
+            nc.tensor.matmul(bank[:], lhsT=neg_ident_bf[:], rhs=x_sb[(j, 1)][:, cols], start=False, stop=True)
+            nc.scalar.copy(out=blend[j][:, cols], in_=bank[:])
 
         def job_z(j, k):
             n = P * SIZES[j]
@@ -468,6 +470,8 @@ def tile_parentgru_pb_t_kernel(tc, inputs, state, parent_state, c, w_a_w, w_a_b,
                 job_a(job[2], job[1])
             elif kind == "f":
                 job_f(job[3], job[1], job[2])
+            elif kind == "e":
+                job_e(job[2], job[1])
             elif kind == "s":
                 job_s(job[3], job[1], job[2])
             else:

@@ -13,293 +13,145 @@ ALU = mybir.AluOpType
 
 P = 128
 B, K, H = 4096, 512, 512
-SIZES = (2, 2, 2, 2, 4, 4, 4, 4, 4, 2, 2)
 FLOPS = 2 * B * 3 * K * H
-
-PIN = True
-XBUFS, STBUFS, CBUFS, GBUFS, QBUFS, BLBUFS, ABUFS = 3, 6, 4, 2, 3, 5, 3
-PLAN = (
-    ('Lw', 0),
-    ('Lw', 1),
-    ('Lw', 2),
-    ('Lx', 0, 0),
-    ('Lx', 1, 0),
-    ('Lx', 2, 0),
-    ('Lc', 0),
-    ('Lx', 1, 1),
-    ('Lc', 1),
-    ('Lx', 0, 1),
-    ('Lx', 2, 1),
-    ('Lx', 1, 2),
-    ('Lc', 2),
-    ('Lx', 0, 2),
-    ('Lx', 2, 2),
-    ('b',),
-    ('w', 0, 0, False),
-    ('w', 0, 1, True),
-    ('W', 0),
-    ('w', 1, 0, False),
-    ('w', 1, 1, True),
-    ('W', 1),
-    ('w', 2, 0, False),
-    ('w', 2, 1, True),
-    ('W', 2),
-    ('x', 0, 0, 0, False),
-    ('q', 0, 0),
-    ('x', 1, 0, 0, False),
-    ('q', 1, 0),
-    ('x', 2, 0, 0, False),
-    ('q', 2, 0),
-    ('x', 0, 0, 1, False),
-    ('x', 1, 0, 1, False),
-    ('q', 0, 1),
-    ('x', 2, 0, 1, False),
-    ('q', 1, 1),
-    ('q', 2, 1),
-    ('d', 0, 2, 0, False),
-    ('d', 0, 2, 1, False),
-    ('Lx', 1, 3),
-    ('Lc', 3),
-    ('Lx', 0, 3),
-    ('Lx', 2, 3),
-    ('d', 0, 2, 2, False),
-    ('z', 0, 0),
-    ('x', 0, 0, 2, False),
-    ('z', 1, 0),
-    ('x', 1, 0, 2, False),
-    ('q', 0, 2),
-    ('x', 2, 0, 2, False),
-    ('q', 1, 2),
-    ('Lx', 1, 4),
-    ('Lc', 4),
-    ('Lx', 0, 4),
-    ('Lx', 2, 4),
-    ('d', 0, 2, 3, False),
-    ('z', 0, 1),
-    ('q', 2, 2),
-    ('a', 0, 0),
-    ('x', 0, 0, 3, False),
-    ('z', 1, 1),
-    ('a', 1, 0),
-    ('x', 1, 0, 3, False),
-    ('q', 0, 3),
-    ('f', 0, 1, 0),
-    ('x', 2, 0, 3, False),
-    ('q', 1, 3),
-    ('Lx', 1, 5),
-    ('Lc', 5),
-    ('Lx', 0, 5),
-    ('Lx', 2, 5),
-    ('d', 0, 2, 4, False),
-    ('z', 0, 2),
-    ('q', 2, 3),
-    ('a', 0, 1),
-    ('x', 0, 0, 4, False),
-    ('f', 1, 2, 0),
-    ('s', 0, 2, 0),
-    ('x', 0, 1, 4, False),
-    ('x', 1, 0, 4, False),
-    ('q', 0, 4),
-    ('d', 2, 3, 4, False),
-    ('e', 3, 4),
-    ('z', 1, 2),
-    ('a', 1, 1),
-    ('x', 1, 1, 4, False),
-    ('f', 0, 1, 1),
-    ('x', 2, 0, 4, False),
-    ('q', 1, 4),
-    ('x', 2, 1, 4, False),
-    ('Lx', 1, 6),
-    ('Lc', 6),
-    ('Lx', 0, 6),
-    ('Lx', 2, 6),
-    ('d', 0, 2, 5, False),
-    ('z', 0, 3),
-    ('q', 2, 4),
-    ('a', 0, 2),
-    ('x', 0, 0, 5, False),
-    ('f', 1, 2, 1),
-    ('s', 0, 2, 1),
-    ('x', 0, 1, 5, False),
-    ('x', 1, 0, 5, False),
-    ('q', 0, 5),
-    ('d', 2, 3, 5, False),
-    ('e', 3, 5),
-    ('z', 1, 3),
-    ('a', 1, 2),
-    ('x', 1, 1, 5, False),
-    ('f', 0, 1, 2),
-    ('x', 2, 0, 5, False),
-    ('q', 1, 5),
-    ('x', 2, 1, 5, False),
-    ('Lx', 1, 7),
-    ('Lc', 7),
-    ('Lx', 0, 7),
-    ('Lx', 2, 7),
-    ('d', 0, 2, 6, False),
-    ('z', 0, 4),
-    ('q', 2, 5),
-    ('x', 0, 0, 6, False),
-    ('z', 1, 4),
-    ('a', 0, 3),
-    ('x', 0, 1, 6, False),
-    ('f', 1, 2, 2),
-    ('s', 0, 2, 2),
-    ('x', 1, 0, 6, False),
-    ('q', 0, 6),
-    ('d', 2, 3, 6, False),
-    ('z', 2, 4),
-    ('x', 1, 1, 6, False),
-    ('e', 3, 6),
-    ('z', 3, 4),
-    ('a', 1, 3),
-    ('x', 2, 0, 6, False),
-    ('q', 1, 6),
-    ('f', 0, 1, 3),
-    ('x', 2, 1, 6, False),
-    ('Lx', 1, 8),
-    ('Lc', 8),
-    ('Lx', 0, 8),
-    ('Lx', 2, 8),
-    ('d', 0, 2, 7, False),
-    ('z', 0, 5),
-    ('q', 2, 6),
-    ('a', 0, 4),
-    ('x', 0, 0, 7, False),
-    ('f', 1, 2, 3),
-    ('s', 0, 2, 3),
-    ('z', 1, 5),
-    ('a', 1, 4),
-    ('x', 0, 1, 7, False),
-    ('f', 0, 1, 4),
-    ('x', 1, 0, 7, False),
-    ('q', 0, 7),
-    ('d', 2, 3, 7, False),
-    ('z', 2, 5),
-    ('a', 2, 4),
-    ('x', 1, 1, 7, False),
-    ('f', 1, 2, 4),
-    ('e', 3, 7),
-    ('z', 3, 5),
-    ('a', 3, 4),
-    ('x', 2, 0, 7, False),
-    ('q', 1, 7),
-    ('f', 2, 3, 4),
-    ('x', 2, 1, 7, False),
-    ('Lx', 1, 9),
-    ('Lc', 9),
-    ('Lx', 0, 9),
-    ('Lx', 2, 9),
-    ('d', 0, 2, 8, False),
-    ('z', 0, 6),
-    ('q', 2, 7),
-    ('a', 0, 5),
-    ('x', 0, 0, 8, False),
-    ('f', 3, 4, 4),
-    ('s', 0, 4, 4),
-    ('z', 1, 6),
-    ('a', 1, 5),
-    ('x', 0, 1, 8, False),
-    ('f', 0, 1, 5),
-    ('x', 1, 0, 8, False),
-    ('q', 0, 8),
-    ('d', 2, 3, 8, False),
-    ('z', 2, 6),
-    ('a', 2, 5),
-    ('x', 1, 1, 8, False),
-    ('f', 1, 2, 5),
-    ('e', 3, 8),
-    ('z', 3, 6),
-    ('a', 3, 5),
-    ('x', 2, 0, 8, False),
-    ('q', 1, 8),
-    ('f', 2, 3, 5),
-    ('x', 2, 1, 8, False),
-    ('Lx', 1, 10),
-    ('Lc', 10),
-    ('Lx', 0, 10),
-    ('Lx', 2, 10),
-    ('z', 0, 7),
-    ('q', 2, 8),
-    ('a', 0, 6),
-    ('f', 3, 4, 5),
-    ('s', 0, 4, 5),
-    ('d', 0, 2, 9, False),
-    ('z', 1, 7),
-    ('a', 1, 6),
-    ('x', 0, 0, 9, False),
-    ('f', 0, 1, 6),
-    ('z', 2, 7),
-    ('a', 2, 6),
-    ('x', 1, 0, 9, False),
-    ('q', 0, 9),
-    ('f', 1, 2, 6),
-    ('z', 3, 7),
-    ('a', 3, 6),
-    ('x', 2, 0, 9, False),
-    ('q', 1, 9),
-    ('f', 2, 3, 6),
-    ('z', 0, 8),
-    ('q', 2, 9),
-    ('a', 0, 7),
-    ('f', 3, 4, 6),
-    ('s', 0, 4, 6),
-    ('d', 0, 2, 10, False),
-    ('z', 1, 8),
-    ('a', 1, 7),
-    ('x', 0, 0, 10, False),
-    ('f', 0, 1, 7),
-    ('z', 2, 8),
-    ('a', 2, 7),
-    ('x', 1, 0, 10, False),
-    ('q', 0, 10),
-    ('f', 1, 2, 7),
-    ('z', 3, 8),
-    ('a', 3, 7),
-    ('x', 2, 0, 10, False),
-    ('q', 1, 10),
-    ('f', 2, 3, 7),
-    ('z', 0, 9),
-    ('q', 2, 10),
-    ('a', 0, 8),
-    ('f', 3, 4, 7),
-    ('s', 0, 4, 7),
-    ('a', 1, 8),
-    ('f', 0, 1, 8),
-    ('z', 1, 9),
-    ('a', 2, 8),
-    ('f', 1, 2, 8),
-    ('a', 3, 8),
-    ('f', 2, 3, 8),
-    ('z', 0, 10),
-    ('a', 0, 9),
-    ('f', 3, 4, 8),
-    ('s', 0, 4, 8),
-    ('z', 1, 10),
-    ('a', 1, 9),
-    ('f', 0, 1, 9),
-    ('s', 0, 1, 9),
-    ('a', 0, 10),
-    ('f', 1, 2, 9),
-    ('s', 1, 2, 9),
-    ('a', 1, 10),
-    ('f', 0, 1, 10),
-    ('s', 0, 1, 10),
-    ('f', 1, 2, 10),
-    ('s', 1, 2, 10),
-)
+PAIRS = 16
+CHUNKS = (1, 1, 2, 2, 2, 2, 2, 2, 1, 1)
+XB, STB, CB, GB, QB, OB, AB, TB = (6, 6, 6, 3, 3, 8, 3, 4)
+AHEAD = 8
+HEAD = (('x', 1, 0), ('c', 0), ('w', 0), ('x', 0, 0), ('w', 1), ('x', 2, 0), ('w', 2))
+GP = (0, 1, 2, 3, 4, 5, 6, 7, 8, 9, 10, 11, 12, 13, 14, 15)
+PE_SUB = ()
+Q_LAG, Z_LAG, A_LAG, F_LAG, D_LAG = (1, 2, 3, 4, 0)
+ORDER = ('f', 'a1', 'a0', 'd1', 'z', 'q0', 'q1', 'q2', 'x0', 'x1', 'x2', 'd0')
 
 
 def tile_parentgru_pb_t_kernel(tc, inputs, state, parent_state, c, w_a_w, w_a_b, u_a_w, p_a_w, out):
     nc = tc.nc
     acts = (inputs, state, parent_state)
     weights = (w_a_w, u_a_w, p_a_w)
+    chunk_of, row0 = {}, {}
+    n = 0
+    for j, size in enumerate(CHUNKS):
+        row0[j] = 2 * P * n
+        for h in range(size):
+            chunk_of[n] = (j, h)
+            n += 1
     with ExitStack() as ctx:
-        if PIN:
-            ctx.enter_context(tc.manual_schedule())
+        ctx.enter_context(tc.manual_schedule())
         const = ctx.enter_context(tc.tile_pool(name="const", bufs=1))
         pool = ctx.enter_context(tc.tile_pool(name="pool", bufs=2))
         psum = ctx.enter_context(tc.psum_pool(name="psum", bufs=8))
+
+        x_sb, c_sb, grouped, codes, planes, diff, att_t, out_sb = {}, {}, {}, {}, {}, {}, {}, {}
+        w_sb, w_grouped, w_codes, w_planes = {}, {}, {}, {}
+
+        def rows(ap, j):
+            r = 2 * CHUNKS[j]
+            return ap[row0[j] : row0[j] + P * r, :].rearrange("(p r) k -> p (r k)", r=r)
+
+        def pair_cols(p):
+            h = chunk_of[p][1]
+            return slice(2 * h * K, 2 * (h + 1) * K)
+
+        def load_w(i):
+            w_sb[i] = const.tile([P, 4 * K], BF16, name="w%d" % i)
+            nc.sync.dma_start(out=w_sb[i][:].rearrange("p (m k) -> p m k", m=4), in_=weights[i].rearrange("(m p) k -> p m k", p=P))
+
+        def load_x(j, i):
+            x_sb[(j, i)] = pool.tile([P, 2 * CHUNKS[j] * K], BF16, name="x%d_%d" % (i, j), tag="x%d" % i, bufs=(STB if i == 1 else XB))
+            nc.sync.dma_start(out=x_sb[(j, i)][:], in_=rows(acts[i], j))
+
+        def load_c(j):
+            c_sb[j] = pool.tile([P, 2 * CHUNKS[j] * K], BF16, name="c_%d" % j, tag="c", bufs=CB)
+            nc.sync.dma_start(out=c_sb[j][:], in_=rows(c, j))
+
+        def flip_out(g, words, half, on_vector):
+            bank = psum.tile([P, 2, 2 * P], F32, name="bank", tag="bank")
+            for rr in range(2):
+                for u in range(2):
+                    col = rr * (K // 2) + u * P
+                    nc.tensor.transpose(bank[:, u, rr * P : (rr + 1) * P], words[:, col : col + P], ident[:])
+            dst = g[:].bitcast(F32).rearrange("q (n u) -> q n u", u=2)[:, half * 2 * P : (half + 1) * 2 * P, :]
+            src = bank[:].rearrange("q u n -> q n u")
+            if on_vector:
+                nc.vector.tensor_copy(out=dst, in_=src)
+            else:
+                nc.scalar.copy(out=dst, in_=src)
+
+        def job_w(i, half, on_vector):
+            if half == 0:
+                w_grouped[i] = pool.tile([P, 4 * H], BF16, name="gw%d" % i, tag="gw", bufs=2, align_bytes=64)
+            flip_out(w_grouped[i], w_sb[i][:, half * 2 * K : (half + 1) * 2 * K].bitcast(F32), half, on_vector)
+
+        def job_qw(i):
+            w_codes[i] = const.tile([P, H], U32, name="wc%d" % i, align_bytes=64)
+            w_planes[i] = const.tile([P, H], U8, name="wp%d" % i, align_bytes=64)
+            nc.vector.quantize_mx(out=w_codes[i][:].bitcast(FP8X4), scales=w_planes[i][:], in_=w_grouped[i][:])
+
+        def job_x(p, i):
+            grouped[(p, i)] = pool.tile([P, 8 * P], BF16, name="g%d_%d" % (i, p), tag="g%d" % i, bufs=GB, align_bytes=64)
+            flip_out(grouped[(p, i)], x_sb[(chunk_of[p][0], i)][:, pair_cols(p)].bitcast(F32), 0, False)
+
+        def job_q(p, i):
+            codes[(p, i)] = pool.tile([P, 2 * P], U32, name="xc%d_%d" % (i, p), tag="xc%d" % i, bufs=QB, align_bytes=64)
+            planes[(p, i)] = pool.tile([P, 2 * P], U8, name="xp%d_%d" % (i, p), tag="xp%d" % i, bufs=QB, align_bytes=64)
+            nc.vector.quantize_mx(out=codes[(p, i)][:].bitcast(FP8X4), scales=planes[(p, i)][:], in_=grouped[(p, i)][:])
+
+        def row_cols(p, r):
+            h = chunk_of[p][1]
+            return slice((2 * h + r) * K, (2 * h + r + 1) * K)
+
+        def job_d(p, r):
+            diff[(p, r)] = pool.tile([P, H], F32, name="t%d_%d" % (r, p), tag="t%d" % r, bufs=TB)
+            j = chunk_of[p][0]
+            if (p, r) in PE_SUB:
+                bank = psum.tile([P, H], F32, name="dbank", tag="bank")
+                nc.tensor.matmul(bank[:], lhsT=ident_bf[:], rhs=c_sb[j][:, row_cols(p, r)], start=True, stop=False)
+                nc.tensor.matmul(bank[:], lhsT=neg_ident_bf[:], rhs=x_sb[(j, 1)][:, row_cols(p, r)], start=False, stop=True)
+                nc.scalar.copy(out=diff[(p, r)][:], in_=bank[:])
+                return
+            eng = nc.gpsimd if (r == 1 and p in GP) else nc.vector
+            eng.tensor_tensor(out=diff[(p, r)][:], in0=c_sb[j][:, row_cols(p, r)], in1=x_sb[(j, 1)][:, row_cols(p, r)], op=ALU.subtract)
+
+        def job_z(p, k):
+            if k == 0:
+                att_t[p] = pool.tile([P, 4, 2 * P], F32, name="a_%d" % p, tag="a", bufs=AB)
+            z = psum.tile([P, 2, 2 * P], F32, name="z", tag="bank")
+            for s in range(2):
+                cols = slice((2 * k + s) * P, (2 * k + s + 1) * P)
+                for i in range(3):
+                    nc.tensor.matmul_mx(
+                        out=z[:, s, :],
+                        lhsT=w_codes[i][:, cols].bitcast(FP8X4),
+                        lhsT_scale=w_planes[i][:, cols],
+                        rhs=codes[(p, i)][:].bitcast(FP8X4),
+                        rhs_scale=planes[(p, i)][:],
+                        start=(i == 0),
+                        stop=(i == 2),
+                    )
+            for s in range(2):
+                t = 2 * k + s
+                nc.scalar.activation(out=att_t[p][:, t, :], in_=z[:, s, :], func=ACT.Sigmoid, bias=bias[:, t : t + 1], scale=1.0)
+
+        def job_a(p, r):
+            bank = psum.tile([P, H], F32, name="att", tag="bank")
+            for t in range(4):
+                nc.tensor.transpose(bank[:, t * P : (t + 1) * P], att_t[p][:, t, r * P : (r + 1) * P], ident[:])
+            nc.vector.tensor_tensor(out=diff[(p, r)][:], in0=bank[:], in1=diff[(p, r)][:], op=ALU.mult)
+
+        def job_f(p, r):
+            j = chunk_of[p][0]
+            if p not in out_sb:
+                out_sb[p] = pool.tile([P, 2 * H], F32, name="o_%d" % p, tag="o", bufs=OB)
+            nc.vector.tensor_tensor(out=out_sb[p][:, r * H : (r + 1) * H], in0=diff[(p, r)][:], in1=x_sb[(j, 1)][:, row_cols(p, r)], op=ALU.add)
+
+        def job_s(p):
+            j = chunk_of[p][0]
+            if p == PAIRS - 1:
+                for r in (1, 0):
+                    nc.sync.dma_start(out=rows(out, j)[:, row_cols(p, r)], in_=out_sb[p][:, r * H : (r + 1) * H])
+            else:
+                nc.sync.dma_start(out=rows(out, j)[:, pair_cols(p)], in_=out_sb[p][:])
 
         ident = const.tile([P, P], F32, name="ident")
         make_identity(nc, ident[:])
@@ -311,175 +163,63 @@ def tile_parentgru_pb_t_kernel(tc, inputs, state, parent_state, c, w_a_w, w_a_b,
         nc.vector.memset(braw[:], 0.0)
         nc.sync.dma_start(out=braw[0:4, :], in_=w_a_b.rearrange("(m p) -> m p", p=P))
         bias = const.tile([P, 4], F32, name="bias")
-
         ident_bf = const.tile([P, P], BF16, name="ident_bf")
         nc.vector.tensor_copy(out=ident_bf[:], in_=ident[:])
         neg_ident_bf = const.tile([P, P], BF16, name="neg_ident_bf")
         nc.vector.tensor_scalar_mul(out=neg_ident_bf[:], in0=ident[:], scalar1=-1.0)
-        x_sb = {}
-        c_sb = {}
-        grouped = {}
-        codes = {}
-        planes = {}
-        blend = {}
-        a_t = {}
-        w_sb = {}
-        w_grouped = {}
-        w_codes = {}
-        w_planes = {}
 
-        first_row = [P * sum(SIZES[:j]) for j in range(len(SIZES))]
-
-        def rows(ap, j):
-            return ap[first_row[j] : first_row[j] + P * SIZES[j], :].rearrange("(p r) k -> p (r k)", r=SIZES[j])
-
-        def load_w(i):
-            t = const.tile([P, 4 * K], BF16, name="w%d" % i)
-            nc.sync.dma_start(out=t[:].rearrange("p (m k) -> p m k", m=4), in_=weights[i].rearrange("(m p) k -> p m k", p=P))
-            w_sb[i] = t
-
-        def load_x(j, i):
-            t = pool.tile([P, SIZES[j] * K], BF16, name="x%d_%d" % (i, j), tag="x%d" % i, bufs=(STBUFS if i == 1 else XBUFS))
-            nc.sync.dma_start(out=t[:], in_=rows(acts[i], j))
-            x_sb[(j, i)] = t
-
-        def load_c(j):
-            t = pool.tile([P, SIZES[j] * K], BF16, name="c_%d" % j, tag="c", bufs=CBUFS)
-            nc.sync.dma_start(out=t[:], in_=rows(c, j))
-            c_sb[j] = t
-
-        def flip_out(g, words, half, on_vector, tiles):
-            bank = psum.tile([P, 2, 2 * P], F32, name="bank", tag="bank")
-            for rr in range(tiles):
-                for u in range(2):
-                    col = (2 * half + rr) * (K // 2) + u * P
-                    nc.tensor.transpose(bank[:, u, rr * P : (rr + 1) * P], words[:, col : col + P], ident[:])
-            dst = g[:].bitcast(F32).rearrange("q (n u) -> q n u", u=2)[:, half * 2 * P : half * 2 * P + tiles * P, :]
-            src = bank[:, :, 0 : tiles * P].rearrange("q u n -> q n u")
-            if on_vector:
-                nc.vector.tensor_copy(out=dst, in_=src)
+        for step in HEAD:
+            if step[0] == "w":
+                load_w(step[1])
+            elif step[0] == "x":
+                load_x(step[2], step[1])
             else:
-                nc.scalar.copy(out=dst, in_=src)
+                load_c(step[1])
+        loads = []
+        for j in range(len(CHUNKS)):
+            for item in (("x", 1, j), ("c", j), ("x", 0, j), ("x", 2, j)):
+                if item not in HEAD:
+                    loads.append(item)
 
-        def job_w(i, half, on_vector):
-            if half == 0:
-                w_grouped[i] = pool.tile([P, 4 * H], BF16, name="gw%d" % i, tag="gw", bufs=2, align_bytes=64)
-            flip_out(w_grouped[i], w_sb[i][:].bitcast(F32), half, on_vector, 2)
+        def load_upto(p):
+            while loads:
+                j = loads[0][-1]
+                if row0[j] > 2 * P * p:
+                    return
+                item = loads.pop(0)
+                if item[0] == "x":
+                    load_x(item[2], item[1])
+                else:
+                    load_c(item[1])
 
-        def job_qw(i):
-            w_codes[i] = const.tile([P, H], U32, name="wc%d" % i, align_bytes=64)
-            w_planes[i] = const.tile([P, H], U8, name="wp%d" % i, align_bytes=64)
-            nc.vector.quantize_mx(out=w_codes[i][:].bitcast(FP8X4), scales=w_planes[i][:], in_=w_grouped[i][:])
+        bf = const.tile([P, P], F32, name="bf")
+        nc.vector.tensor_copy(out=bf[:], in_=braw[:])
+        bbank = psum.tile([P, 2, 2 * P], F32, name="bbank", tag="bank")
+        nc.tensor.transpose(bbank[:, 0, 0:P], bf[:], ident[:])
+        nc.vector.tensor_copy(out=bias[:], in_=bbank[:, 0, 0:4])
+        for i in range(3):
+            job_w(i, 0, False)
+            job_w(i, 1, True)
+            job_qw(i)
 
-        def job_x(j, i, half, on_vector):
-            if half == 0:
-                grouped[(j, i)] = pool.tile([P, 4 * P * SIZES[j]], BF16, name="g%d_%d" % (i, j), tag="g%d" % i, bufs=GBUFS, align_bytes=64)
-            flip_out(grouped[(j, i)], x_sb[(j, i)][:].bitcast(F32), half, on_vector, min(2, SIZES[j] - 2 * half))
-
-        def job_q(j, i):
-            codes[(j, i)] = pool.tile([P, P * SIZES[j]], U32, name="xc%d_%d" % (i, j), tag="xc%d" % i, bufs=QBUFS, align_bytes=64)
-            planes[(j, i)] = pool.tile([P, P * SIZES[j]], U8, name="xp%d_%d" % (i, j), tag="xp%d" % i, bufs=QBUFS, align_bytes=64)
-            nc.vector.quantize_mx(out=codes[(j, i)][:].bitcast(FP8X4), scales=planes[(j, i)][:], in_=grouped[(j, i)][:])
-
-        def job_d(j, r0, r1, on_gpsimd):
-            if j not in blend:
-                blend[j] = pool.tile([P, SIZES[j] * H], F32, name="bl_%d" % j, tag="bl", bufs=BLBUFS)
-            cols = slice(r0 * H, r1 * H)
-            eng = nc.gpsimd if on_gpsimd else nc.vector
-            eng.tensor_tensor(out=blend[j][:, cols], in0=c_sb[j][:, cols], in1=x_sb[(j, 1)][:, cols], op=ALU.subtract)
-
-        def job_e(j, r):
-            if j not in blend:
-                blend[j] = pool.tile([P, SIZES[j] * H], F32, name="bl_%d" % j, tag="bl", bufs=BLBUFS)
-            cols = slice(r * H, (r + 1) * H)
-            bank = psum.tile([P, H], F32, name="dbank", tag="bank")
-            nc.tensor.matmul(bank[:], lhsT=ident_bf[:], rhs=c_sb[j][:, cols], start=True, stop=False)
-            nc.tensor.matmul(bank[:], lhsT=neg_ident_bf[:], rhs=x_sb[(j, 1)][:, cols], start=False, stop=True)
-            nc.scalar.copy(out=blend[j][:, cols], in_=bank[:])
-
-        def job_z(j, k):
-            n = P * SIZES[j]
-            per_bank = 4 // SIZES[j]
-            if k == 0:
-                a_t[j] = pool.tile([P, 4, n], F32, name="a_%d" % j, tag="a", bufs=ABUFS)
-            z = psum.tile([P, 4 * P], F32, name="z", tag="bank")
-            for s in range(per_bank):
-                t = k * per_bank + s
-                cols = slice(t * P, (t + 1) * P)
-                for i in range(3):
-                    nc.tensor.matmul_mx(
-                        out=z[:, s * n : (s + 1) * n],
-                        lhsT=w_codes[i][:, cols].bitcast(FP8X4),
-                        lhsT_scale=w_planes[i][:, cols],
-                        rhs=codes[(j, i)][:].bitcast(FP8X4),
-                        rhs_scale=planes[(j, i)][:],
-                        start=(i == 0),
-                        stop=(i == 2),
-                    )
-            for s in range(per_bank):
-                t = k * per_bank + s
-                nc.scalar.activation(
-                    out=a_t[j][:, t, :], in_=z[:, s * n : (s + 1) * n], func=ACT.Sigmoid, bias=bias[:, t : t + 1], scale=1.0
-                )
-
-        def job_a(j, r):
-            bank = psum.tile([P, H], F32, name="att", tag="bank")
-            for t in range(4):
-                nc.tensor.transpose(bank[:, t * P : (t + 1) * P], a_t[j][:, t, r * P : (r + 1) * P], ident[:])
-            part = blend[j][:, r * H : (r + 1) * H]
-            nc.vector.tensor_tensor(out=part, in0=bank[:], in1=part, op=ALU.mult)
-
-        def job_f(j, r0, r1):
-            cols = slice(r0 * H, r1 * H)
-            nc.vector.tensor_tensor(out=blend[j][:, cols], in0=blend[j][:, cols], in1=x_sb[(j, 1)][:, cols], op=ALU.add)
-
-        def job_s(j, r0, r1):
-            cols = slice(r0 * H, r1 * H)
-            nc.sync.dma_start(out=rows(out, j)[:, cols], in_=blend[j][:, cols])
-
-        def job_bias():
-            bf = const.tile([P, P], F32, name="bf")
-            nc.vector.tensor_copy(out=bf[:], in_=braw[:])
-            bank = psum.tile([P, 2, 2 * P], F32, name="bbank", tag="bank")
-            nc.tensor.transpose(bank[:, 0, 0:P], bf[:], ident[:])
-            nc.vector.tensor_copy(out=bias[:], in_=bank[:, 0, 0:4])
-
-        def run(job):
-            kind = job[0]
-            if kind == "Lw":
-                load_w(job[1])
-            elif kind == "Lx":
-                load_x(job[2], job[1])
-            elif kind == "Lc":
-                load_c(job[1])
-            elif kind == "w":
-                job_w(job[1], job[2], job[3])
-            elif kind == "W":
-                job_qw(job[1])
-            elif kind == "b":
-                job_bias()
-            elif kind == "x":
-                job_x(job[3], job[1], job[2], job[4])
-            elif kind == "q":
-                job_q(job[2], job[1])
-            elif kind == "d":
-                job_d(job[3], job[1], job[2], job[4])
-            elif kind == "z":
-                job_z(job[2], job[1])
-            elif kind == "a":
-                job_a(job[2], job[1])
-            elif kind == "f":
-                job_f(job[3], job[1], job[2])
-            elif kind == "e":
-                job_e(job[2], job[1])
-            elif kind == "s":
-                job_s(job[3], job[1], job[2])
-            else:
-                raise ValueError(kind)
-
-        for job in make_plan():
-            run(job)
-
-
-def make_plan():
-    return PLAN
+        for s in range(PAIRS + F_LAG):
+            load_upto(s + AHEAD)
+            px, pq, pz, pa, pf, pd = s, s - Q_LAG, s - Z_LAG, s - A_LAG, s - F_LAG, s - D_LAG
+            for step in ORDER:
+                if step == "z" and 0 <= pz < PAIRS:
+                    job_z(pz, 0)
+                    job_z(pz, 1)
+                elif step in ("z0", "z1") and 0 <= pz < PAIRS:
+                    job_z(pz, int(step[1]))
+                elif step == "f" and 0 <= pf < PAIRS:
+                    job_f(pf, 1)
+                    job_f(pf, 0)
+                    job_s(pf)
+                elif step in ("d0", "d1") and 0 <= pd < PAIRS:
+                    job_d(pd, int(step[1]))
+                elif step in ("a0", "a1") and 0 <= pa < PAIRS:
+                    job_a(pa, int(step[1]))
+                elif step in ("x0", "x1", "x2") and px < PAIRS:
+                    job_x(px, int(step[1]))
+                elif step in ("q0", "q1", "q2") and 0 <= pq < PAIRS:
+                    job_q(pq, int(step[1]))

@@ -15,14 +15,17 @@ P = 128
 B, K, H = 4096, 512, 512
 FLOPS = 2 * B * 3 * K * H
 PAIRS = 16
-CHUNKS = (1, 1, 2, 2, 2, 2, 2, 2, 1, 1)
+CHUNKS = (1, 1, 1, 1, 2, 2, 2, 2, 2, 1, 1)
 XB, STB, CB, GB, QB, OB, AB, TB = (6, 6, 6, 3, 3, 8, 3, 4)
 AHEAD = 8
 HEAD = (('x', 1, 0), ('c', 0), ('w', 0), ('x', 0, 0), ('w', 1), ('x', 2, 0), ('w', 2))
-GP = (0, 1, 2, 3, 4, 5, 6, 7, 8, 9, 10, 11, 12, 13, 14, 15)
+GP = (3, 4, 5, 6, 7, 8, 9, 10, 11, 12, 13, 14, 15)
 PE_SUB = ()
 Q_LAG, Z_LAG, A_LAG, F_LAG, D_LAG = (1, 2, 3, 4, 0)
 ORDER = ('f', 'a1', 'a0', 'd1', 'z', 'q0', 'q1', 'q2', 'x0', 'x1', 'x2', 'd0')
+TAIL_ORDER = ('f', 'a1', 'a0', 'z', 'q0', 'q1', 'q2')
+HJOBS = (('d', 0, 0), ('d', 0, 1), ('x', 1, 0, False), ('w', 0, 0, False), ('q', 1, 0), ('w', 0, 1, True), ('W', 0), ('x', 0, 0, False), ('w', 1, 0, False), ('w', 1, 1, True), ('q', 0, 0), ('W', 1), ('x', 2, 0, False), ('w', 2, 0, False), ('w', 2, 1, True), ('q', 2, 0), ('W', 2))
+S0 = 0
 
 
 def tile_parentgru_pb_t_kernel(tc, inputs, state, parent_state, c, w_a_w, w_a_b, u_a_w, p_a_w, out):
@@ -88,9 +91,9 @@ def tile_parentgru_pb_t_kernel(tc, inputs, state, parent_state, c, w_a_w, w_a_b,
             w_planes[i] = const.tile([P, H], U8, name="wp%d" % i, align_bytes=64)
             nc.vector.quantize_mx(out=w_codes[i][:].bitcast(FP8X4), scales=w_planes[i][:], in_=w_grouped[i][:])
 
-        def job_x(p, i):
+        def job_x(p, i, on_vector=False):
             grouped[(p, i)] = pool.tile([P, 8 * P], BF16, name="g%d_%d" % (i, p), tag="g%d" % i, bufs=GB, align_bytes=64)
-            flip_out(grouped[(p, i)], x_sb[(chunk_of[p][0], i)][:, pair_cols(p)].bitcast(F32), 0, False)
+            flip_out(grouped[(p, i)], x_sb[(chunk_of[p][0], i)][:, pair_cols(p)].bitcast(F32), 0, on_vector)
 
         def job_q(p, i):
             codes[(p, i)] = pool.tile([P, 2 * P], U32, name="xc%d_%d" % (i, p), tag="xc%d" % i, bufs=QB, align_bytes=64)
@@ -139,11 +142,12 @@ def tile_parentgru_pb_t_kernel(tc, inputs, state, parent_state, c, w_a_w, w_a_b,
                 nc.tensor.transpose(bank[:, t * P : (t + 1) * P], att_t[p][:, t, r * P : (r + 1) * P], ident[:])
             nc.vector.tensor_tensor(out=diff[(p, r)][:], in0=bank[:], in1=diff[(p, r)][:], op=ALU.mult)
 
-        def job_f(p, r):
+        def job_f(p, r, on_gpsimd=False):
             j = chunk_of[p][0]
             if p not in out_sb:
                 out_sb[p] = pool.tile([P, 2 * H], F32, name="o_%d" % p, tag="o", bufs=OB)
-            nc.vector.tensor_tensor(out=out_sb[p][:, r * H : (r + 1) * H], in0=diff[(p, r)][:], in1=x_sb[(j, 1)][:, row_cols(p, r)], op=ALU.add)
+            eng = nc.gpsimd if on_gpsimd else nc.vector
+            eng.tensor_tensor(out=out_sb[p][:, r * H : (r + 1) * H], in0=diff[(p, r)][:], in1=x_sb[(j, 1)][:, row_cols(p, r)], op=ALU.add)
 
         def job_s(p):
             j = chunk_of[p][0]
@@ -197,15 +201,22 @@ def tile_parentgru_pb_t_kernel(tc, inputs, state, parent_state, c, w_a_w, w_a_b,
         bbank = psum.tile([P, 2, 2 * P], F32, name="bbank", tag="bank")
         nc.tensor.transpose(bbank[:, 0, 0:P], bf[:], ident[:])
         nc.vector.tensor_copy(out=bias[:], in_=bbank[:, 0, 0:4])
-        for i in range(3):
-            job_w(i, 0, False)
-            job_w(i, 1, True)
-            job_qw(i)
+        for step in HJOBS:
+            if step[0] == "w":
+                job_w(step[1], step[2], step[3])
+            elif step[0] == "W":
+                job_qw(step[1])
+            elif step[0] == "x":
+                job_x(step[2], step[1], step[3])
+            elif step[0] == "q":
+                job_q(step[2], step[1])
+            elif step[0] == "d":
+                job_d(step[1], step[2])
 
-        for s in range(PAIRS + F_LAG):
+        for s in range(S0, PAIRS + F_LAG):
             load_upto(s + AHEAD)
             px, pq, pz, pa, pf, pd = s, s - Q_LAG, s - Z_LAG, s - A_LAG, s - F_LAG, s - D_LAG
-            for step in ORDER:
+            for step in (TAIL_ORDER if s >= PAIRS else ORDER):
                 if step == "z" and 0 <= pz < PAIRS:
                     job_z(pz, 0)
                     job_z(pz, 1)
@@ -215,11 +226,15 @@ def tile_parentgru_pb_t_kernel(tc, inputs, state, parent_state, c, w_a_w, w_a_b,
                     job_f(pf, 1)
                     job_f(pf, 0)
                     job_s(pf)
-                elif step in ("d0", "d1") and 0 <= pd < PAIRS:
+                elif step in ("f0", "f1", "g0", "g1") and 0 <= pf < PAIRS:
+                    job_f(pf, int(step[1]), step[0] == "g" and pf < PAIRS - 1)
+                elif step == "s" and 0 <= pf < PAIRS:
+                    job_s(pf)
+                elif step in ("d0", "d1") and 0 <= pd < PAIRS and (pd, int(step[1])) not in diff:
                     job_d(pd, int(step[1]))
                 elif step in ("a0", "a1") and 0 <= pa < PAIRS:
                     job_a(pa, int(step[1]))
-                elif step in ("x0", "x1", "x2") and px < PAIRS:
+                elif step in ("x0", "x1", "x2") and px < PAIRS and (px, int(step[1])) not in grouped:
                     job_x(px, int(step[1]))
-                elif step in ("q0", "q1", "q2") and 0 <= pq < PAIRS:
+                elif step in ("q0", "q1", "q2") and 0 <= pq < PAIRS and (pq, int(step[1])) not in codes:
                     job_q(pq, int(step[1]))

@@ -18,14 +18,21 @@ PAIRS = 16
 CHUNKS = (1, 1, 1, 1, 2, 2, 2, 2, 2, 1, 1)
 XB, STB, CB, GB, QB, OB, AB, TB = (6, 6, 6, 3, 3, 8, 3, 4)
 AHEAD = 8
-HEAD = (('x', 1, 0), ('c', 0), ('w', 0), ('x', 0, 0), ('w', 1), ('x', 2, 0), ('w', 2))
+HEAD = (('w', 0), ('w', 1), ('w', 2), ('x', 1, 0), ('x', 0, 0), ('x', 2, 0), ('b',), ('c', 0))
 GP = (3, 4, 5, 6, 7, 8, 9, 10, 11, 12, 13, 14, 15)
 PE_SUB = ()
 Q_LAG, Z_LAG, A_LAG, F_LAG, D_LAG = (1, 2, 3, 4, 0)
-ORDER = ('f', 'a1', 'a0', 'd1', 'z', 'q0', 'q1', 'q2', 'x0', 'x1', 'x2', 'd0')
-TAIL_ORDER = ('f', 'a1', 'a0', 'z', 'q0', 'q1', 'q2')
-HJOBS = (('d', 0, 0), ('d', 0, 1), ('x', 1, 0, False), ('w', 0, 0, False), ('q', 1, 0), ('w', 0, 1, True), ('W', 0), ('x', 0, 0, False), ('w', 1, 0, False), ('w', 1, 1, True), ('q', 0, 0), ('W', 1), ('x', 2, 0, False), ('w', 2, 0, False), ('w', 2, 1, True), ('q', 2, 0), ('W', 2))
-S0 = 0
+ORDER = ('f', 'a1', 'a0', 'd1', 'z', 'q1', 'q0', 'q2', 'x1', 'x0', 'x2', 'd0')
+TAIL_ORDER = (('e0', 'e1', 'f', 'a1', 'a0', 'z', 'q0', 'q1', 'q2'),)
+HEAD_ORDER = ()
+HEAD_SLOTS = 0
+SP = 1
+E_LAG = 2
+HJOBS = (('w', 0, 0, False), ('w', 0, 1, True), ('w', 1, 0, False), ('W', 0), ('w', 1, 1, True), ('w', 2, 0, False), ('W', 1), ('w', 2, 1, True), ('x', 1, 0, False), ('W', 2), ('q', 1, 0), ('x', 0, 0, False), ('q', 0, 0), ('x', 2, 0, False), ('q', 2, 0), ('b',), ('d', 0, 0), ('d', 0, 1), ('x', 1, 1, False), ('z', 0))
+S0 = 1
+C_BEHIND = 0
+C_POS = 1
+SPLIT_STORE = 15
 
 
 def tile_parentgru_pb_t_kernel(tc, inputs, state, parent_state, c, w_a_w, w_a_b, u_a_w, p_a_w, out):
@@ -58,7 +65,7 @@ def tile_parentgru_pb_t_kernel(tc, inputs, state, parent_state, c, w_a_w, w_a_b,
 
         def load_w(i):
             w_sb[i] = const.tile([P, 4 * K], BF16, name="w%d" % i)
-            nc.sync.dma_start(out=w_sb[i][:].rearrange("p (m k) -> p m k", m=4), in_=weights[i].rearrange("(m p) k -> p m k", p=P))
+            nc.sync.dma_start(out=w_sb[i][:], in_=weights[i].rearrange("(p m) k -> p (m k)", m=4))
 
         def load_x(j, i):
             x_sb[(j, i)] = pool.tile([P, 2 * CHUNKS[j] * K], BF16, name="x%d_%d" % (i, j), tag="x%d" % i, bufs=(STB if i == 1 else XB))
@@ -113,7 +120,7 @@ def tile_parentgru_pb_t_kernel(tc, inputs, state, parent_state, c, w_a_w, w_a_b,
                 nc.tensor.matmul(bank[:], lhsT=neg_ident_bf[:], rhs=x_sb[(j, 1)][:, row_cols(p, r)], start=False, stop=True)
                 nc.scalar.copy(out=diff[(p, r)][:], in_=bank[:])
                 return
-            eng = nc.gpsimd if (r == 1 and p in GP) else nc.vector
+            eng = nc.gpsimd if ((p, r) in GP or (r == 1 and p in GP)) else nc.vector
             eng.tensor_tensor(out=diff[(p, r)][:], in0=c_sb[j][:, row_cols(p, r)], in1=x_sb[(j, 1)][:, row_cols(p, r)], op=ALU.subtract)
 
         def job_z(p, k):
@@ -136,11 +143,15 @@ def tile_parentgru_pb_t_kernel(tc, inputs, state, parent_state, c, w_a_w, w_a_b,
                 t = 2 * k + s
                 nc.scalar.activation(out=att_t[p][:, t, :], in_=z[:, s, :], func=ACT.Sigmoid, bias=bias[:, t : t + 1], scale=1.0)
 
+        done_a = set()
+
         def job_a(p, r):
+            done_a.add((p, r))
             bank = psum.tile([P, H], F32, name="att", tag="bank")
             for t in range(4):
                 nc.tensor.transpose(bank[:, t * P : (t + 1) * P], att_t[p][:, t, r * P : (r + 1) * P], ident[:])
-            nc.vector.tensor_tensor(out=diff[(p, r)][:], in0=bank[:], in1=diff[(p, r)][:], op=ALU.mult)
+            part = diff[(p, r)][:].rearrange("p (q t) -> p q t", t=4)
+            nc.vector.tensor_tensor(out=part, in0=bank[:].rearrange("p (t q) -> p q t", t=4), in1=part, op=ALU.mult)
 
         def job_f(p, r, on_gpsimd=False):
             j = chunk_of[p][0]
@@ -151,7 +162,7 @@ def tile_parentgru_pb_t_kernel(tc, inputs, state, parent_state, c, w_a_w, w_a_b,
 
         def job_s(p):
             j = chunk_of[p][0]
-            if p == PAIRS - 1:
+            if p >= SPLIT_STORE:
                 for r in (1, 0):
                     nc.sync.dma_start(out=rows(out, j)[:, row_cols(p, r)], in_=out_sb[p][:, r * H : (r + 1) * H])
             else:
@@ -163,9 +174,7 @@ def tile_parentgru_pb_t_kernel(tc, inputs, state, parent_state, c, w_a_w, w_a_b,
         warmed = const.tile([P, 1], F32, name="warmed")
         nc.vector.memset(warm[:], 0.0)
         nc.scalar.activation(out=warmed[:], in_=warm[:], func=ACT.Sigmoid)
-        braw = const.tile([P, P], BF16, name="braw")
-        nc.vector.memset(braw[:], 0.0)
-        nc.sync.dma_start(out=braw[0:4, :], in_=w_a_b.rearrange("(m p) -> m p", p=P))
+        braw = const.tile([P, 4], BF16, name="braw")
         bias = const.tile([P, 4], F32, name="bias")
         ident_bf = const.tile([P, P], BF16, name="ident_bf")
         nc.vector.tensor_copy(out=ident_bf[:], in_=ident[:])
@@ -173,22 +182,30 @@ def tile_parentgru_pb_t_kernel(tc, inputs, state, parent_state, c, w_a_w, w_a_b,
         nc.vector.tensor_scalar_mul(out=neg_ident_bf[:], in0=ident[:], scalar1=-1.0)
 
         for step in HEAD:
-            if step[0] == "w":
+            if step[0] == "b":
+                nc.sync.dma_start(out=braw[:], in_=w_a_b.rearrange("(q t) -> q t", t=4))
+            elif step[0] == "w":
                 load_w(step[1])
             elif step[0] == "x":
                 load_x(step[2], step[1])
             else:
                 load_c(step[1])
         loads = []
-        for j in range(len(CHUNKS)):
-            for item in (("x", 1, j), ("c", j), ("x", 0, j), ("x", 2, j)):
+        n_ch = len(CHUNKS)
+        for j in range(n_ch + C_BEHIND):
+            items = []
+            if j < n_ch:
+                items += [("x", 1, j), ("x", 0, j), ("x", 2, j)]
+            if j >= C_BEHIND:
+                items.insert(min(len(items), C_POS), ("c", j - C_BEHIND))
+            for item in items:
                 if item not in HEAD:
                     loads.append(item)
 
         def load_upto(p):
             while loads:
-                j = loads[0][-1]
-                if row0[j] > 2 * P * p:
+                j = loads[0][-1] + (C_BEHIND if loads[0][0] == "c" else 0)
+                if j < n_ch and row0[j] > 2 * P * p:
                     return
                 item = loads.pop(0)
                 if item[0] == "x":
@@ -196,11 +213,7 @@ def tile_parentgru_pb_t_kernel(tc, inputs, state, parent_state, c, w_a_w, w_a_b,
                 else:
                     load_c(item[1])
 
-        bf = const.tile([P, P], F32, name="bf")
-        nc.vector.tensor_copy(out=bf[:], in_=braw[:])
-        bbank = psum.tile([P, 2, 2 * P], F32, name="bbank", tag="bank")
-        nc.tensor.transpose(bbank[:, 0, 0:P], bf[:], ident[:])
-        nc.vector.tensor_copy(out=bias[:], in_=bbank[:, 0, 0:4])
+        load_upto(S0 - 1 + AHEAD)
         for step in HJOBS:
             if step[0] == "w":
                 job_w(step[1], step[2], step[3])
@@ -212,15 +225,27 @@ def tile_parentgru_pb_t_kernel(tc, inputs, state, parent_state, c, w_a_w, w_a_b,
                 job_q(step[2], step[1])
             elif step[0] == "d":
                 job_d(step[1], step[2])
+            elif step[0] == "b":
+                nc.vector.tensor_copy(out=bias[:], in_=braw[:])
+            elif step[0] == "z":
+                job_z(step[1], 0)
+                job_z(step[1], 1)
+            elif step[0] == "a":
+                job_a(step[1], step[2])
+            elif step[0] == "L":
+                load_upto(step[1])
 
-        for s in range(S0, PAIRS + F_LAG):
-            load_upto(s + AHEAD)
-            px, pq, pz, pa, pf, pd = s, s - Q_LAG, s - Z_LAG, s - A_LAG, s - F_LAG, s - D_LAG
-            for step in (TAIL_ORDER if s >= PAIRS else ORDER):
-                if step == "z" and 0 <= pz < PAIRS:
+        for s0 in range(S0, PAIRS + F_LAG, SP):
+            load_upto(s0 + SP - 1 + AHEAD)
+            for step in (TAIL_ORDER[min(s0 - PAIRS, len(TAIL_ORDER) - 1)] if s0 >= PAIRS else HEAD_ORDER if s0 < HEAD_SLOTS else ORDER):
+                s = s0
+                while step[0] == "+":
+                    s, step = s + 1, step[1:]
+                px, pq, pz, pa, pf, pd = s, s - Q_LAG, s - Z_LAG, s - A_LAG, s - F_LAG, s - D_LAG
+                if step == "z" and 0 <= pz < PAIRS and (pz not in att_t or step == "z1"):
                     job_z(pz, 0)
                     job_z(pz, 1)
-                elif step in ("z0", "z1") and 0 <= pz < PAIRS:
+                elif step in ("z0", "z1") and 0 <= pz < PAIRS and (pz not in att_t or step == "z1"):
                     job_z(pz, int(step[1]))
                 elif step == "f" and 0 <= pf < PAIRS:
                     job_f(pf, 1)
@@ -228,11 +253,13 @@ def tile_parentgru_pb_t_kernel(tc, inputs, state, parent_state, c, w_a_w, w_a_b,
                     job_s(pf)
                 elif step in ("f0", "f1", "g0", "g1") and 0 <= pf < PAIRS:
                     job_f(pf, int(step[1]), step[0] == "g" and pf < PAIRS - 1)
+                elif step in ("e0", "e1") and 0 <= s - E_LAG < PAIRS and (s - E_LAG, int(step[1])) in PE_SUB:
+                    job_d(s - E_LAG, int(step[1]))
                 elif step == "s" and 0 <= pf < PAIRS:
                     job_s(pf)
-                elif step in ("d0", "d1") and 0 <= pd < PAIRS and (pd, int(step[1])) not in diff:
+                elif step in ("d0", "d1") and 0 <= pd < PAIRS and (pd, int(step[1])) not in diff and (pd, int(step[1])) not in PE_SUB:
                     job_d(pd, int(step[1]))
-                elif step in ("a0", "a1") and 0 <= pa < PAIRS:
+                elif step in ("a0", "a1") and 0 <= pa < PAIRS and (pa, int(step[1])) not in done_a:
                     job_a(pa, int(step[1]))
                 elif step in ("x0", "x1", "x2") and px < PAIRS and (px, int(step[1])) not in grouped:
                     job_x(px, int(step[1]))

@@ -18,18 +18,18 @@ PAIRS = 16
 CHUNKS = (1, 1, 1, 1, 2, 2, 2, 2, 2, 1, 1)
 XB, STB, CB, GB, QB, OB, AB, TB = (6, 6, 6, 3, 3, 8, 3, 4)
 AHEAD = 8
-HEAD = (('w', 0), ('w', 1), ('w', 2), ('x', 1, 0), ('x', 0, 0), ('x', 2, 0), ('b',), ('c', 0))
+HEAD = (('b',), ('x', 1, 0), ('c', 0), ('w', 0), ('x', 0, 0), ('w', 1), ('x', 2, 0), ('w', 2))
 GP = (3, 4, 5, 6, 7, 8, 9, 10, 11, 12, 13, 14, 15)
 PE_SUB = ()
 Q_LAG, Z_LAG, A_LAG, F_LAG, D_LAG = (1, 2, 3, 4, 0)
-ORDER = ('f', 'a1', 'a0', 'd1', 'z', 'q1', 'q0', 'q2', 'x1', 'x0', 'x2', 'd0')
+ORDER = ('f', 'a1', 'a0', 'd1', 'z', 'q0', 'q1', 'q2', 'x0', 'x1', 'x2', 'd0')
 TAIL_ORDER = (('e0', 'e1', 'f', 'a1', 'a0', 'z', 'q0', 'q1', 'q2'),)
 HEAD_ORDER = ()
 HEAD_SLOTS = 0
 SP = 1
 E_LAG = 2
-HJOBS = (('w', 0, 0, False), ('w', 0, 1, True), ('w', 1, 0, False), ('W', 0), ('w', 1, 1, True), ('w', 2, 0, False), ('W', 1), ('w', 2, 1, True), ('x', 1, 0, False), ('W', 2), ('q', 1, 0), ('x', 0, 0, False), ('q', 0, 0), ('x', 2, 0, False), ('q', 2, 0), ('b',), ('d', 0, 0), ('d', 0, 1), ('x', 1, 1, False), ('z', 0))
-S0 = 1
+HJOBS = (('b',), ('d', 0, 0), ('d', 0, 1), ('x', 1, 0, False), ('w', 0, 0, False), ('q', 1, 0), ('w', 0, 1, True), ('W', 0), ('x', 0, 0, False), ('w', 1, 0, False), ('w', 1, 1, True), ('q', 0, 0), ('W', 1), ('x', 2, 0, False), ('w', 2, 0, False), ('w', 2, 1, True), ('q', 2, 0), ('W', 2))
+S0 = 0
 C_BEHIND = 0
 C_POS = 1
 SPLIT_STORE = 15

@@ -20,10 +20,10 @@ XB, STB, CB, GB, QB, OB, AB, TB = (6, 6, 6, 3, 3, 8, 3, 4)
 AHEAD = 8
 HEAD = (('b',), ('x', 1, 0), ('c', 0), ('w', 0), ('x', 0, 0), ('w', 1), ('x', 2, 0), ('w', 2))
 GP = (3, 4, 5, 6, 7, 8, 9, 10, 11, 12, 13, 14, 15)
-PE_SUB = ()
+PE_SUB = ((14, 0), (15, 0))
 Q_LAG, Z_LAG, A_LAG, F_LAG, D_LAG = (1, 2, 3, 4, 0)
 ORDER = ('f', 'a1', 'a0', 'd1', 'z', 'q0', 'q1', 'q2', 'x0', 'x1', 'x2', 'd0')
-TAIL_ORDER = (('e0', 'e1', 'f', 'a1', 'a0', 'z', 'q0', 'q1', 'q2'),)
+TAIL_ORDER = (('f', 'a1', 'a0', 'z', 'e0', 'q0', 'q1', 'q2'),)
 HEAD_ORDER = ()
 HEAD_SLOTS = 0
 SP = 1
@@ -176,6 +176,9 @@ def tile_parentgru_pb_t_kernel(tc, inputs, state, parent_state, c, w_a_w, w_a_b,
         nc.scalar.activation(out=warmed[:], in_=warm[:], func=ACT.Sigmoid)
         braw = const.tile([P, 4], BF16, name="braw")
         bias = const.tile([P, 4], F32, name="bias")
+        if any(step[0] == "k" for step in HJOBS):
+            idle = const.tile([P, H], BF16, name="idle_sb")
+            nc.vector.memset(idle[:], 0.0)
         ident_bf = const.tile([P, P], BF16, name="ident_bf")
         nc.vector.tensor_copy(out=ident_bf[:], in_=ident[:])
         neg_ident_bf = const.tile([P, P], BF16, name="neg_ident_bf")
@@ -214,6 +217,11 @@ def tile_parentgru_pb_t_kernel(tc, inputs, state, parent_state, c, w_a_w, w_a_b,
                     load_c(item[1])
 
         load_upto(S0 - 1 + AHEAD)
+        def job_k(n):
+            bank = psum.tile([P, H], F32, name="idle", tag="bank")
+            for m in range(n):
+                nc.tensor.matmul(bank[:], lhsT=idle[:, 0:P], rhs=idle[:], start=True, stop=True)
+
         for step in HJOBS:
             if step[0] == "w":
                 job_w(step[1], step[2], step[3])
@@ -225,6 +233,8 @@ def tile_parentgru_pb_t_kernel(tc, inputs, state, parent_state, c, w_a_w, w_a_b,
                 job_q(step[2], step[1])
             elif step[0] == "d":
                 job_d(step[1], step[2])
+            elif step[0] == "k":
+                job_k(step[1])
             elif step[0] == "b":
                 nc.vector.tensor_copy(out=bias[:], in_=braw[:])
             elif step[0] == "z":

@@ -20,16 +20,17 @@ XB, STB, CB, GB, QB, OB, AB, TB = (6, 6, 6, 3, 3, 8, 3, 4)
 AHEAD = 8
 HEAD = (('b',), ('x', 1, 0), ('c', 0), ('w', 0), ('x', 0, 0), ('w', 1), ('x', 2, 0), ('w', 2))
 GP = (3, 4, 5, 6, 7, 8, 9, 10, 11, 12, 13, 14, 15)
-PE_SUB = ((14, 0), (15, 0))
+PE_SUB = ((4, 0), (6, 0), (8, 0), (10, 0), (12, 0), (14, 0), (15, 0))
 Q_LAG, Z_LAG, A_LAG, F_LAG, D_LAG = (1, 2, 3, 4, 0)
-ORDER = ('f', 'a1', 'a0', 'd1', 'z', 'q0', 'q1', 'q2', 'x0', 'x1', 'x2', 'd0')
-TAIL_ORDER = (('f', 'a1', 'a0', 'z', 'e0', 'q0', 'q1', 'q2'),)
+ORDER = ('f', 'a1', 'a0', 'd1', 'z', 'e0', 'e1', 'q0', 'q1', 'q2', 'x0', 'x1', 'x2', 'd0')
+TAIL_ORDER = (('f', 'a1', 'a0', 'z', 'e0', 'e1', 'q0', 'q1', 'q2'),)
 HEAD_ORDER = ()
 HEAD_SLOTS = 0
 SP = 1
 E_LAG = 2
 HJOBS = (('b',), ('d', 0, 0), ('d', 0, 1), ('x', 1, 0, False), ('w', 0, 0, False), ('q', 1, 0), ('w', 0, 1, True), ('W', 0), ('x', 0, 0, False), ('w', 1, 0, False), ('w', 1, 1, True), ('q', 0, 0), ('W', 1), ('x', 2, 0, False), ('w', 2, 0, False), ('w', 2, 1, True), ('q', 2, 0), ('W', 2))
 S0 = 0
+VPIECE = 0
 C_BEHIND = 0
 C_POS = 1
 SPLIT_STORE = 15
@@ -120,8 +121,16 @@ def tile_parentgru_pb_t_kernel(tc, inputs, state, parent_state, c, w_a_w, w_a_b,
                 nc.tensor.matmul(bank[:], lhsT=neg_ident_bf[:], rhs=x_sb[(j, 1)][:, row_cols(p, r)], start=False, stop=True)
                 nc.scalar.copy(out=diff[(p, r)][:], in_=bank[:])
                 return
-            eng = nc.gpsimd if ((p, r) in GP or (r == 1 and p in GP)) else nc.vector
-            eng.tensor_tensor(out=diff[(p, r)][:], in0=c_sb[j][:, row_cols(p, r)], in1=x_sb[(j, 1)][:, row_cols(p, r)], op=ALU.subtract)
+            lo, hi = row_cols(p, r).start, row_cols(p, r).stop
+            eng = nc.vector
+            if (p, r) in GP or (r == 1 and p in GP):
+                eng = nc.gpsimd
+                if VPIECE:
+                    nc.vector.tensor_tensor(out=diff[(p, r)][:, 0:VPIECE], in0=c_sb[j][:, lo : lo + VPIECE], in1=x_sb[(j, 1)][:, lo : lo + VPIECE], op=ALU.subtract)
+            else:
+                assert True
+            cut = VPIECE if eng is nc.gpsimd else 0
+            eng.tensor_tensor(out=diff[(p, r)][:, cut:H], in0=c_sb[j][:, lo + cut : hi], in1=x_sb[(j, 1)][:, lo + cut : hi], op=ALU.subtract)
 
         def job_z(p, k):
             if k == 0:

@@ -20,17 +20,20 @@ XB, STB, CB, GB, QB, OB, AB, TB = (6, 6, 6, 3, 3, 8, 3, 4)
 AHEAD = 8
 HEAD = (('b',), ('x', 1, 0), ('c', 0), ('w', 0), ('x', 0, 0), ('w', 1), ('x', 2, 0), ('w', 2))
 GP = (3, 4, 5, 6, 7, 8, 9, 10, 11, 12, 13, 14, 15)
-PE_SUB = ((4, 0), (6, 0), (8, 0), (10, 0), (12, 0), (14, 0), (15, 0))
+PE_SUB = ((14, 0), (15, 0))
+PE_PART = (4, 5, 6, 7, 8, 9, 10, 11, 12, 13)
+ECOLS = 256
 Q_LAG, Z_LAG, A_LAG, F_LAG, D_LAG = (1, 2, 3, 4, 0)
-ORDER = ('f', 'a1', 'a0', 'd1', 'z', 'e0', 'e1', 'q0', 'q1', 'q2', 'x0', 'x1', 'x2', 'd0')
-TAIL_ORDER = (('f', 'a1', 'a0', 'z', 'e0', 'e1', 'q0', 'q1', 'q2'),)
+ORDER = ('f', 'a1', 'a0', 'd1', 'z', 'h0', 'e0', 'e1', 'q1', 'q0', 'q2', 'x1', 'x0', 'x2', 'd0')
+TAIL_ORDER = (('f', 'a1', 'a0', 'z', 'h0', 'e0', 'q1', 'q0', 'q2'),)
 HEAD_ORDER = ()
 HEAD_SLOTS = 0
 SP = 1
 E_LAG = 2
+H_LAG = 1
 HJOBS = (('b',), ('d', 0, 0), ('d', 0, 1), ('x', 1, 0, False), ('w', 0, 0, False), ('q', 1, 0), ('w', 0, 1, True), ('W', 0), ('x', 0, 0, False), ('w', 1, 0, False), ('w', 1, 1, True), ('q', 0, 0), ('W', 1), ('x', 2, 0, False), ('w', 2, 0, False), ('w', 2, 1, True), ('q', 2, 0), ('W', 2))
 S0 = 0
-VPIECE = 0
+VPIECE = 128
 C_BEHIND = 0
 C_POS = 1
 SPLIT_STORE = 15
@@ -112,14 +115,24 @@ def tile_parentgru_pb_t_kernel(tc, inputs, state, parent_state, c, w_a_w, w_a_b,
             h = chunk_of[p][1]
             return slice((2 * h + r) * K, (2 * h + r + 1) * K)
 
+        def job_e(p, r, n):
+            j = chunk_of[p][0]
+            lo = row_cols(p, r).start
+            bank = psum.tile([P, n], F32, name="dbank", tag="bank")
+            nc.tensor.matmul(bank[:], lhsT=ident_bf[:], rhs=c_sb[j][:, lo : lo + n], start=True, stop=False)
+            nc.tensor.matmul(bank[:], lhsT=neg_ident_bf[:], rhs=x_sb[(j, 1)][:, lo : lo + n], start=False, stop=True)
+            nc.scalar.copy(out=diff[(p, r)][:, 0:n], in_=bank[:])
+
         def job_d(p, r):
             diff[(p, r)] = pool.tile([P, H], F32, name="t%d_%d" % (r, p), tag="t%d" % r, bufs=TB)
             j = chunk_of[p][0]
             if (p, r) in PE_SUB:
-                bank = psum.tile([P, H], F32, name="dbank", tag="bank")
-                nc.tensor.matmul(bank[:], lhsT=ident_bf[:], rhs=c_sb[j][:, row_cols(p, r)], start=True, stop=False)
-                nc.tensor.matmul(bank[:], lhsT=neg_ident_bf[:], rhs=x_sb[(j, 1)][:, row_cols(p, r)], start=False, stop=True)
-                nc.scalar.copy(out=diff[(p, r)][:], in_=bank[:])
+                job_e(p, r, H)
+                return
+            if r == 0 and p in PE_PART:
+                job_e(p, r, ECOLS)
+                lo, hi = row_cols(p, r).start, row_cols(p, r).stop
+                nc.vector.tensor_tensor(out=diff[(p, r)][:, ECOLS:H], in0=c_sb[j][:, lo + ECOLS : hi], in1=x_sb[(j, 1)][:, lo + ECOLS : hi], op=ALU.subtract)
                 return
             lo, hi = row_cols(p, r).start, row_cols(p, r).stop
             eng = nc.vector
@@ -272,11 +285,13 @@ def tile_parentgru_pb_t_kernel(tc, inputs, state, parent_state, c, w_a_w, w_a_b,
                     job_s(pf)
                 elif step in ("f0", "f1", "g0", "g1") and 0 <= pf < PAIRS:
                     job_f(pf, int(step[1]), step[0] == "g" and pf < PAIRS - 1)
+                elif step == "h0" and 0 <= s - H_LAG < PAIRS and s - H_LAG in PE_PART and (s - H_LAG, 0) not in diff:
+                    job_d(s - H_LAG, 0)
                 elif step in ("e0", "e1") and 0 <= s - E_LAG < PAIRS and (s - E_LAG, int(step[1])) in PE_SUB:
                     job_d(s - E_LAG, int(step[1]))
                 elif step == "s" and 0 <= pf < PAIRS:
                     job_s(pf)
-                elif step in ("d0", "d1") and 0 <= pd < PAIRS and (pd, int(step[1])) not in diff and (pd, int(step[1])) not in PE_SUB:
+                elif step in ("d0", "d1") and 0 <= pd < PAIRS and (pd, int(step[1])) not in diff and (pd, int(step[1])) not in PE_SUB and not (step == "d0" and pd in PE_PART):
                     job_d(pd, int(step[1]))
                 elif step in ("a0", "a1") and 0 <= pa < PAIRS and (pa, int(step[1])) not in done_a:
                     job_a(pa, int(step[1]))

@@ -31,7 +31,7 @@ HEAD_SLOTS = 0
 SP = 1
 E_LAG = 2
 H_LAG = 1
-HJOBS = (('b',), ('d', 0, 0), ('d', 0, 1), ('x', 1, 0, False), ('w', 0, 0, False), ('q', 1, 0), ('w', 0, 1, True), ('W', 0), ('x', 0, 0, False), ('w', 1, 0, False), ('w', 1, 1, True), ('q', 0, 0), ('W', 1), ('x', 2, 0, False), ('w', 2, 0, False), ('w', 2, 1, True), ('q', 2, 0), ('W', 2))
+HJOBS = (('k', 4), ('b',), ('d', 0, 0), ('d', 0, 1), ('x', 1, 0, False), ('k', 2), ('w', 0, 0, False), ('q', 1, 0), ('w', 0, 1, True), ('W', 0), ('x', 0, 0, False), ('k', 2), ('w', 1, 0, False), ('w', 1, 1, True), ('q', 0, 0), ('W', 1), ('x', 2, 0, False), ('k', 2), ('w', 2, 0, False), ('w', 2, 1, True), ('q', 2, 0), ('W', 2), ('k', 2))
 S0 = 0
 VPIECE = 128
 C_BEHIND = 0

from contextlib import ExitStack

import concourse.mybir as mybir
from concourse.masks import make_identity

F32 = mybir.dt.float32
BF16 = mybir.dt.bfloat16
U32 = mybir.dt.uint32
U8 = mybir.dt.uint8
FP8X4 = mybir.dt.float8_e4m3fn_x4
ACT = mybir.ActivationFunctionType
ALU = mybir.AluOpType

P = 128
B, K, H = 4096, 512, 512
FLOPS = 2 * B * 3 * K * H
PAIRS = 16
CHUNKS = (1, 1, 1, 1, 2, 2, 2, 2, 2, 1, 1)
XB, STB, CB, GB, QB, OB, AB, TB = (6, 6, 6, 3, 3, 8, 3, 4)
AHEAD = 8
HEAD = (('b',), ('x', 1, 0), ('c', 0), ('w', 0), ('x', 0, 0), ('w', 1), ('x', 2, 0), ('w', 2))
GP = (3, 4, 5, 6, 7, 8, 9, 10, 11, 12, 13, 14, 15)
PE_SUB = ((14, 0), (15, 0))
PE_PART = (4, 5, 6, 7, 8, 9, 10, 11, 12, 13)
ECOLS = 256
Q_LAG, Z_LAG, A_LAG, F_LAG, D_LAG = (1, 2, 3, 4, 0)
ORDER = ('f', 'a1', 'a0', 'd1', 'z', 'h0', 'e0', 'e1', 'q1', 'q0', 'q2', 'x1', 'x0', 'x2', 'd0')
TAIL_ORDER = (('f', 'a1', 'a0', 'z', 'h0', 'e0', 'q1', 'q0', 'q2'),)
HEAD_ORDER = ()
HEAD_SLOTS = 0
SP = 1
E_LAG = 2
H_LAG = 1
HJOBS = (('k', 4), ('b',), ('d', 0, 0), ('d', 0, 1), ('x', 1, 0, False), ('k', 2), ('w', 0, 0, False), ('q', 1, 0), ('w', 0, 1, True), ('W', 0), ('x', 0, 0, False), ('k', 2), ('w', 1, 0, False), ('w', 1, 1, True), ('q', 0, 0), ('W', 1), ('x', 2, 0, False), ('k', 2), ('w', 2, 0, False), ('w', 2, 1, True), ('q', 2, 0), ('W', 2), ('k', 2))
S0 = 0
VPIECE = 128
C_BEHIND = 0
C_POS = 1
SPLIT_STORE = 15


def tile_parentgru_pb_t_kernel(tc, inputs, state, parent_state, c, w_a_w, w_a_b, u_a_w, p_a_w, out):
    nc = tc.nc
    acts = (inputs, state, parent_state)
    weights = (w_a_w, u_a_w, p_a_w)
    chunk_of, row0 = {}, {}
    n = 0
    for j, size in enumerate(CHUNKS):
        row0[j] = 2 * P * n
        for h in range(size):
            chunk_of[n] = (j, h)
            n += 1
    with ExitStack() as ctx:
        ctx.enter_context(tc.manual_schedule())
        const = ctx.enter_context(tc.tile_pool(name="const", bufs=1))
        pool = ctx.enter_context(tc.tile_pool(name="pool", bufs=2))
        psum = ctx.enter_context(tc.psum_pool(name="psum", bufs=8))

        x_sb, c_sb, grouped, codes, planes, diff, att_t, out_sb = {}, {}, {}, {}, {}, {}, {}, {}
        w_sb, w_grouped, w_codes, w_planes = {}, {}, {}, {}

        def rows(ap, j):
            r = 2 * CHUNKS[j]
            return ap[row0[j] : row0[j] + P * r, :].rearrange("(p r) k -> p (r k)", r=r)

        def pair_cols(p):
            h = chunk_of[p][1]
            return slice(2 * h * K, 2 * (h + 1) * K)

        def load_w(i):
            w_sb[i] = const.tile([P, 4 * K], BF16, name="w%d" % i)
            nc.sync.dma_start(out=w_sb[i][:], in_=weights[i].rearrange("(p m) k -> p (m k)", m=4))

        def load_x(j, i):
            x_sb[(j, i)] = pool.tile([P, 2 * CHUNKS[j] * K], BF16, name="x%d_%d" % (i, j), tag="x%d" % i, bufs=(STB if i == 1 else XB))
            nc.sync.dma_start(out=x_sb[(j, i)][:], in_=rows(acts[i], j))

        def load_c(j):
            c_sb[j] = pool.tile([P, 2 * CHUNKS[j] * K], BF16, name="c_%d" % j, tag="c", bufs=CB)
            nc.sync.dma_start(out=c_sb[j][:], in_=rows(c, j))

        def flip_out(g, words, half, on_vector):
            bank = psum.tile([P, 2, 2 * P], F32, name="bank", tag="bank")
            for rr in range(2):
                for u in range(2):
                    col = rr * (K // 2) + u * P
                    nc.tensor.transpose(bank[:, u, rr * P : (rr + 1) * P], words[:, col : col + P], ident[:])
            dst = g[:].bitcast(F32).rearrange("q (n u) -> q n u", u=2)[:, half * 2 * P : (half + 1) * 2 * P, :]
            src = bank[:].rearrange("q u n -> q n u")
            if on_vector:
                nc.vector.tensor_copy(out=dst, in_=src)
            else:
                nc.scalar.copy(out=dst, in_=src)

        def job_w(i, half, on_vector):
            if half == 0:
                w_grouped[i] = pool.tile([P, 4 * H], BF16, name="gw%d" % i, tag="gw", bufs=2, align_bytes=64)
            flip_out(w_grouped[i], w_sb[i][:, half * 2 * K : (half + 1) * 2 * K].bitcast(F32), half, on_vector)

        def job_qw(i):
            w_codes[i] = const.tile([P, H], U32, name="wc%d" % i, align_bytes=64)
            w_planes[i] = const.tile([P, H], U8, name="wp%d" % i, align_bytes=64)
            nc.vector.quantize_mx(out=w_codes[i][:].bitcast(FP8X4), scales=w_planes[i][:], in_=w_grouped[i][:])

        def job_x(p, i, on_vector=False):
            grouped[(p, i)] = pool.tile([P, 8 * P], BF16, name="g%d_%d" % (i, p), tag="g%d" % i, bufs=GB, align_bytes=64)
            flip_out(grouped[(p, i)], x_sb[(chunk_of[p][0], i)][:, pair_cols(p)].bitcast(F32), 0, on_vector)

        def job_q(p, i):
            codes[(p, i)] = pool.tile([P, 2 * P], U32, name="xc%d_%d" % (i, p), tag="xc%d" % i, bufs=QB, align_bytes=64)
            planes[(p, i)] = pool.tile([P, 2 * P], U8, name="xp%d_%d" % (i, p), tag="xp%d" % i, bufs=QB, align_bytes=64)
            nc.vector.quantize_mx(out=codes[(p, i)][:].bitcast(FP8X4), scales=planes[(p, i)][:], in_=grouped[(p, i)][:])

        def row_cols(p, r):
            h = chunk_of[p][1]
            return slice((2 * h + r) * K, (2 * h + r + 1) * K)

        def job_e(p, r, n):
            j = chunk_of[p][0]
            lo = row_cols(p, r).start
            bank = psum.tile([P, n], F32, name="dbank", tag="bank")
            nc.tensor.matmul(bank[:], lhsT=ident_bf[:], rhs=c_sb[j][:, lo : lo + n], start=True, stop=False)
            nc.tensor.matmul(bank[:], lhsT=neg_ident_bf[:], rhs=x_sb[(j, 1)][:, lo : lo + n], start=False, stop=True)
            nc.scalar.copy(out=diff[(p, r)][:, 0:n], in_=bank[:])

        def job_d(p, r):
            diff[(p, r)] = pool.tile([P, H], F32, name="t%d_%d" % (r, p), tag="t%d" % r, bufs=TB)
            j = chunk_of[p][0]
            if (p, r) in PE_SUB:
                job_e(p, r, H)
                return
            if r == 0 and p in PE_PART:
                job_e(p, r, ECOLS)
                lo, hi = row_cols(p, r).start, row_cols(p, r).stop
                nc.vector.tensor_tensor(out=diff[(p, r)][:, ECOLS:H], in0=c_sb[j][:, lo + ECOLS : hi], in1=x_sb[(j, 1)][:, lo + ECOLS : hi], op=ALU.subtract)
                return
            lo, hi = row_cols(p, r).start, row_cols(p, r).stop
            eng = nc.vector
            if (p, r) in GP or (r == 1 and p in GP):
                eng = nc.gpsimd
                if VPIECE:
                    nc.vector.tensor_tensor(out=diff[(p, r)][:, 0:VPIECE], in0=c_sb[j][:, lo : lo + VPIECE], in1=x_sb[(j, 1)][:, lo : lo + VPIECE], op=ALU.subtract)
            else:
                assert True
            cut = VPIECE if eng is nc.gpsimd else 0
            eng.tensor_tensor(out=diff[(p, r)][:, cut:H], in0=c_sb[j][:, lo + cut : hi], in1=x_sb[(j, 1)][:, lo + cut : hi], op=ALU.subtract)

        def job_z(p, k):
            if k == 0:
                att_t[p] = pool.tile([P, 4, 2 * P], F32, name="a_%d" % p, tag="a", bufs=AB)
            z = psum.tile([P, 2, 2 * P], F32, name="z", tag="bank")
            for s in range(2):
                cols = slice((2 * k + s) * P, (2 * k + s + 1) * P)
                for i in range(3):
                    nc.tensor.matmul_mx(
                        out=z[:, s, :],
                        lhsT=w_codes[i][:, cols].bitcast(FP8X4),
                        lhsT_scale=w_planes[i][:, cols],
                        rhs=codes[(p, i)][:].bitcast(FP8X4),
                        rhs_scale=planes[(p, i)][:],
                        start=(i == 0),
                        stop=(i == 2),
                    )
            for s in range(2):
                t = 2 * k + s
                nc.scalar.activation(out=att_t[p][:, t, :], in_=z[:, s, :], func=ACT.Sigmoid, bias=bias[:, t : t + 1], scale=1.0)

        done_a = set()

        def job_a(p, r):
            done_a.add((p, r))
            bank = psum.tile([P, H], F32, name="att", tag="bank")
            for t in range(4):
                nc.tensor.transpose(bank[:, t * P : (t + 1) * P], att_t[p][:, t, r * P : (r + 1) * P], ident[:])
            part = diff[(p, r)][:].rearrange("p (q t) -> p q t", t=4)
            nc.vector.tensor_tensor(out=part, in0=bank[:].rearrange("p (t q) -> p q t", t=4), in1=part, op=ALU.mult)

        def job_f(p, r, on_gpsimd=False):
            j = chunk_of[p][0]
            if p not in out_sb:
                out_sb[p] = pool.tile([P, 2 * H], F32, name="o_%d" % p, tag="o", bufs=OB)
            eng = nc.gpsimd if on_gpsimd else nc.vector
            eng.tensor_tensor(out=out_sb[p][:, r * H : (r + 1) * H], in0=diff[(p, r)][:], in1=x_sb[(j, 1)][:, row_cols(p, r)], op=ALU.add)

        def job_s(p):
            j = chunk_of[p][0]
            if p >= SPLIT_STORE:
                for r in (1, 0):
                    nc.sync.dma_start(out=rows(out, j)[:, row_cols(p, r)], in_=out_sb[p][:, r * H : (r + 1) * H])
            else:
                nc.sync.dma_start(out=rows(out, j)[:, pair_cols(p)], in_=out_sb[p][:])

        ident = const.tile([P, P], F32, name="ident")
        make_identity(nc, ident[:])
        warm = const.tile([P, 1], F32, name="warm")
        warmed = const.tile([P, 1], F32, name="warmed")
        nc.vector.memset(warm[:], 0.0)
        nc.scalar.activation(out=warmed[:], in_=warm[:], func=ACT.Sigmoid)
        braw = const.tile([P, 4], BF16, name="braw")
        bias = const.tile([P, 4], F32, name="bias")
        if any(step[0] == "k" for step in HJOBS):
            idle = const.tile([P, H], BF16, name="idle_sb")
            nc.vector.memset(idle[:], 0.0)
        ident_bf = const.tile([P, P], BF16, name="ident_bf")
        nc.vector.tensor_copy(out=ident_bf[:], in_=ident[:])
        neg_ident_bf = const.tile([P, P], BF16, name="neg_ident_bf")
        nc.vector.tensor_scalar_mul(out=neg_ident_bf[:], in0=ident[:], scalar1=-1.0)

        for step in HEAD:
            if step[0] == "b":
                nc.sync.dma_start(out=braw[:], in_=w_a_b.rearrange("(q t) -> q t", t=4))
            elif step[0] == "w":
                load_w(step[1])
            elif step[0] == "x":
                load_x(step[2], step[1])
            else:
                load_c(step[1])
        loads = []
        n_ch = len(CHUNKS)
        for j in range(n_ch + C_BEHIND):
            items = []
            if j < n_ch:
                items += [("x", 1, j), ("x", 0, j), ("x", 2, j)]
            if j >= C_BEHIND:
                items.insert(min(len(items), C_POS), ("c", j - C_BEHIND))
            for item in items:
                if item not in HEAD:
                    loads.append(item)

        def load_upto(p):
            while loads:
                j = loads[0][-1] + (C_BEHIND if loads[0][0] == "c" else 0)
                if j < n_ch and row0[j] > 2 * P * p:
                    return
                item = loads.pop(0)
                if item[0] == "x":
                    load_x(item[2], item[1])
                else:
                    load_c(item[1])

        load_upto(S0 - 1 + AHEAD)
        def job_k(n):
            bank = psum.tile([P, H], F32, name="idle", tag="bank")
            for m in range(n):
                nc.tensor.matmul(bank[:], lhsT=idle[:, 0:P], rhs=idle[:], start=True, stop=True)

        for step in HJOBS:
            if step[0] == "w":
                job_w(step[1], step[2], step[3])
            elif step[0] == "W":
                job_qw(step[1])
            elif step[0] == "x":
                job_x(step[2], step[1], step[3])
            elif step[0] == "q":
                job_q(step[2], step[1])
            elif step[0] == "d":
                job_d(step[1], step[2])
            elif step[0] == "k":
                job_k(step[1])
            elif step[0] == "b":
                nc.vector.tensor_copy(out=bias[:], in_=braw[:])
            elif step[0] == "z":
                job_z(step[1], 0)
                job_z(step[1], 1)
            elif step[0] == "a":
                job_a(step[1], step[2])
            elif step[0] == "L":
                load_upto(step[1])

        for s0 in range(S0, PAIRS + F_LAG, SP):
            load_upto(s0 + SP - 1 + AHEAD)
            for step in (TAIL_ORDER[min(s0 - PAIRS, len(TAIL_ORDER) - 1)] if s0 >= PAIRS else HEAD_ORDER if s0 < HEAD_SLOTS else ORDER):
                s = s0
                while step[0] == "+":
                    s, step = s + 1, step[1:]
                px, pq, pz, pa, pf, pd = s, s - Q_LAG, s - Z_LAG, s - A_LAG, s - F_LAG, s - D_LAG
                if step == "z" and 0 <= pz < PAIRS and (pz not in att_t or step == "z1"):
                    job_z(pz, 0)
                    job_z(pz, 1)
                elif step in ("z0", "z1") and 0 <= pz < PAIRS and (pz not in att_t or step == "z1"):
                    job_z(pz, int(step[1]))
                elif step == "f" and 0 <= pf < PAIRS:
                    job_f(pf, 1)
                    job_f(pf, 0)
                    job_s(pf)
                elif step in ("f0", "f1", "g0", "g1") and 0 <= pf < PAIRS:
                    job_f(pf, int(step[1]), step[0] == "g" and pf < PAIRS - 1)
                elif step == "h0" and 0 <= s - H_LAG < PAIRS and s - H_LAG in PE_PART and (s - H_LAG, 0) not in diff:
                    job_d(s - H_LAG, 0)
                elif step in ("e0", "e1") and 0 <= s - E_LAG < PAIRS and (s - E_LAG, int(step[1])) in PE_SUB:
                    job_d(s - E_LAG, int(step[1]))
                elif step == "s" and 0 <= pf < PAIRS:
                    job_s(pf)
                elif step in ("d0", "d1") and 0 <= pd < PAIRS and (pd, int(step[1])) not in diff and (pd, int(step[1])) not in PE_SUB and not (step == "d0" and pd in PE_PART):
                    job_d(pd, int(step[1]))
                elif step in ("a0", "a1") and 0 <= pa < PAIRS and (pa, int(step[1])) not in done_a:
                    job_a(pa, int(step[1]))
                elif step in ("x0", "x1", "x2") and px < PAIRS and (px, int(step[1])) not in grouped:
                    job_x(px, int(step[1]))
                elif step in ("q0", "q1", "q2") and 0 <= pq < PAIRS and (pq, int(step[1])) not in codes:
                    job_q(pq, int(step[1]))
